import numpy as np
import ml_dtypes


def mxq(x, axis, fmt="e4m3"):
    dtype, down = {"e4m3": (ml_dtypes.float8_e4m3fn, 7), "e5m2": (ml_dtypes.float8_e5m2, 14)}[fmt]
    v = np.moveaxis(np.asarray(x, np.float32).astype(ml_dtypes.bfloat16).astype(np.float64), axis, -1)
    blocks = v.reshape(v.shape[:-1] + (-1, 32))
    amax = np.abs(blocks).max(-1, keepdims=True)
    byte = np.maximum(np.where(amax > 0, np.frexp(amax)[1] - 1 + 127, 0) - down, 1)
    scale = np.exp2(byte - 127.0)
    codes = (blocks / scale).astype(np.float32).astype(dtype).astype(np.float64)
    return np.moveaxis((codes * scale).reshape(v.shape), -1, axis)


WIDE = False


def mx_kscale(k):
    if not WIDE:
        return np.ones(k)
    levels = np.array([10, -10, 5, -5, 0])
    a = np.random.permutation(np.resize(levels, k // 512 * 4)).reshape(k // 512, 4)
    idx = np.arange(k)
    return np.exp2(a[idx // 512, idx % 128 // 32])


BF16 = ml_dtypes.bfloat16


def bf(x):
    return np.asarray(x, np.float32).astype(BF16)


def f64(x):
    return np.asarray(x).astype(np.float64)


B, S, E, H, C = 1, 512, 2048, 16, 512
HD = E // H
EPS = 1e-5


def silu(v):
    return v / (1.0 + np.exp(-v))


def setup_inputs():
    s, t = mx_kscale(E), mx_kscale(E)
    spread = np.exp(0.7 * np.random.standard_normal((B, S, H, 1)))
    shift = 0.5 * np.random.standard_normal((B, S, H, 1))
    attn = 1.5 * (np.random.standard_normal((B, S, H, HD)) * spread + shift)
    return {"x": bf(np.random.standard_normal((B, S, E)) * s),
            "attn": bf(attn.reshape(B, S, E)),
            "Wg": bf(np.random.standard_normal((E, E)) / np.sqrt(E) / s[:, None]),
            "bg": bf(np.random.standard_normal(E) * 0.2),
            "gn_w": bf((1.0 + 0.1 * np.random.standard_normal(E)) * t),
            "gn_b": bf(0.1 * np.random.standard_normal(E) * t),
            "Wo": bf(np.random.standard_normal((E, E)) * 1.5 / np.sqrt(E) / t[:, None]),
            "bo": bf(np.random.standard_normal(E) * 0.1)}


def reference(x, attn, Wg, bg, gn_w, gn_b, Wo, bo):
    g = f64(attn).reshape(B, S, H, HD)
    mu = g.mean(-1, keepdims=True)
    var = g.var(-1, keepdims=True)
    g = (g - mu) / np.sqrt(var + EPS)
    g = g.reshape(B, S, E) * f64(gn_w) + f64(gn_b)
    gate = silu((mxq(f64(x), 2, "e4m3") @ mxq(f64(Wg), 0, "e4m3")) + f64(bg))
    h = gate * g
    return (mxq(h, 2, "e4m3") @ mxq(f64(Wo), 0, "e4m3")) + f64(bo)

@@ -1,0 +1,344 @@
+from contextlib import ExitStack
+
+import concourse.mybir as mybir
+from concourse.masks import make_identity
+
+F32 = mybir.dt.float32
+BF16 = mybir.dt.bfloat16
+U32 = mybir.dt.uint32
+U8 = mybir.dt.uint8
+FP8X4 = mybir.dt.float8_e4m3fn_x4
+ALU = mybir.AluOpType
+ACT = mybir.ActivationFunctionType
+
+P = 128
+S = 512
+E = 2048
+EPS = 1e-5
+NPASS = E // 512
+FLOPS = 2 * 2 * S * E * E
+
+ORDER = [
+    ("ldA", 0), ("ld", "g", 0, 0), ("bn", 0), ("ldA", 1), ("ld", "g", 0, 1), ("RGS", "g", 1, 0),
+    ("RGV", "g", 0, 0), ("bn", 1), ("ldA", 2), ("ld", "g", 0, 2), ("RGS", "g", 0, 1), ("Q", "g", 0, 0),
+    ("Q", "g", 1, 0), ("ldA", 3), ("bn", 2), ("RGS", "g", 1, 1), ("ld", "g", 0, 3), ("Q", "g", 0, 1),
+    ("RGS", "g", 0, 2), ("Q", "g", 1, 1), ("ld", "x", 0, 0), ("bn", 3), ("RGS", "g", 1, 2), ("ld", "x", 1, 0),
+    ("sm",), ("Q", "g", 0, 2), ("sqrt",), ("Q", "g", 1, 2), ("RGS", "g", 0, 3), ("recip",), ("J4", 0, 0),
+    ("xT", 0, 0), ("ld", "g", 1, 0), ("xT", 1, 0), ("J4", 0, 1), ("xT", 2, 0), ("xT", 3, 0), ("J4", 0, 2),
+    ("XE", 0, 0), ("Q", "g", 0, 3), ("XE", 1, 0), ("J4", 0, 3), ("xT", 0, 1), ("XE", 2, 0), ("ld", "g", 1, 1),
+    ("xT", 1, 1), ("XE", 0, 1), ("J4", 1, 0), ("xT", 2, 1), ("xT", 3, 1), ("XE", 1, 1), ("J4", 1, 1),
+    ("T", 0, 0), ("XE", 2, 1), ("T", 0, 1), ("Qx", 0), ("XE", 3, 0), ("T", 0, 2), ("Qx", 1),
+    ("ld", "g", 1, 2), ("XE", 3, 1), ("Qx", 2), ("GW", 0, 0), ("T", 0, 3), ("Qx", 3), ("GW", 0, 1),
+    ("J4", 1, 2), ("GW", 0, 2), ("MX1", 0, 0), ("J4", 1, 3), ("ld", "g", 1, 3), ("GW", 0, 3),
+    ("RGV", "g", 2, 0), ("MX1", 0, 1), ("RGS", "g", 1, 3), ("Q", "g", 2, 0), ("MX1", 0, 2), ("J4", 2, 0),
+    ("ldbo",), ("RGV", "g", 2, 2), ("MX1", 0, 3), ("SIL", 0, 0), ("SIL", 0, 1), ("ld", "o", 0, 0),
+    ("Q", "g", 1, 3), ("T", 1, 0), ("SIL", 0, 2), ("T", 1, 1), ("Q", "g", 2, 2), ("T", 1, 2), ("SIL", 0, 3),
+    ("T", 1, 3), ("RGV", "g", 2, 3), ("MX1", 1, 0), ("GW", 1, 0), ("GW", 1, 1), ("ld", "o", 0, 1), ("MUL", 0),
+    ("MX1", 1, 1), ("GW", 1, 2), ("SIL", 1, 0), ("MX1", 1, 2), ("SIL", 1, 1), ("GW", 1, 3), ("QH", 0),
+    ("MX1", 1, 3), ("SIL", 1, 2), ("Q", "g", 2, 3), ("RGS", "g", 2, 1), ("J4", 2, 1), ("J4", 2, 2),
+    ("J4", 2, 3), ("RGV", "g", 3, 2), ("T", 2, 0), ("SIL", 1, 3), ("T", 2, 1), ("GW", 2, 0), ("T", 2, 2),
+    ("ld", "o", 0, 2), ("MUL", 1), ("T", 2, 3), ("GW", 2, 1), ("GW", 2, 2), ("GW", 2, 3), ("RGS", "g", 3, 0),
+    ("QH", 1), ("Q", "g", 2, 1), ("Q", "g", 3, 2), ("MX1", 2, 0), ("RGV", "g", 3, 3), ("ld", "o", 0, 3),
+    ("RGS", "g", 3, 1), ("MX1", 2, 1), ("Q", "g", 3, 0), ("Q", "g", 3, 3), ("MX1", 2, 2), ("J4", 3, 0),
+    ("SIL", 2, 0), ("ld", "o", 1, 0), ("Q", "g", 3, 1), ("SIL", 2, 1), ("MX1", 2, 3), ("J4", 3, 1),
+    ("SIL", 2, 2), ("J4", 3, 2), ("MX1", 3, 0), ("RGS", "o", 0, 0), ("J4", 3, 3), ("ld", "o", 1, 1),
+    ("MX1", 3, 1), ("RGV", "o", 0, 2), ("SIL", 2, 3), ("T", 3, 0), ("Q", "o", 0, 0), ("T", 3, 1),
+    ("SIL", 3, 0), ("T", 3, 2), ("MUL", 2), ("T", 3, 3), ("GW", 3, 0), ("MX1", 3, 2), ("SIL", 3, 1),
+    ("GW", 3, 1), ("MX1", 3, 3), ("QH", 2), ("SIL", 3, 2), ("Q", "o", 0, 2), ("MX2", 0, 0), ("GW", 3, 2),
+    ("RGV", "o", 1, 2), ("SIL", 3, 3), ("GW", 3, 3), ("ld", "o", 1, 2), ("Q", "o", 1, 2), ("RGS", "o", 0, 1),
+    ("MUL", 3), ("RGS", "o", 0, 3), ("QH", 3), ("Q", "o", 0, 1), ("RGV", "o", 2, 0), ("MX2", 0, 1),
+    ("RGS", "o", 1, 0), ("Q", "o", 0, 3), ("MX2", 0, 2), ("Q", "o", 2, 0), ("RGV", "o", 3, 0), ("MX2", 0, 3),
+    ("ld", "o", 1, 3), ("RGS", "o", 1, 1), ("Q", "o", 1, 0), ("J5", 0, 0), ("MX2", 1, 0), ("J5", 0, 1),
+    ("RGS", "o", 1, 3), ("J5", 0, 2), ("st", 0, 0), ("MX2", 2, 0), ("Q", "o", 1, 1), ("st", 0, 1),
+    ("J5", 0, 3), ("st", 0, 2), ("MX2", 1, 1), ("Q", "o", 3, 0), ("RGS", "o", 2, 1), ("st", 0, 3),
+    ("Q", "o", 1, 3), ("MX2", 1, 2), ("RGV", "o", 3, 1), ("MX2", 1, 3), ("Q", "o", 3, 1), ("RGS", "o", 2, 2),
+    ("Q", "o", 2, 1), ("J5", 1, 0), ("MX2", 2, 1), ("J5", 1, 1), ("st", 1, 0), ("RGS", "o", 2, 3),
+    ("J5", 1, 2), ("st", 1, 1), ("MX2", 3, 0), ("J5", 1, 3), ("st", 1, 2), ("Q", "o", 2, 2), ("st", 1, 3),
+    ("MX2", 3, 1), ("RGV", "o", 3, 3), ("RGS", "o", 3, 2), ("MX2", 2, 2), ("Q", "o", 2, 3), ("Q", "o", 3, 3),
+    ("MX2", 2, 3), ("Q", "o", 3, 2), ("J5", 2, 0), ("MX2", 3, 2), ("J5", 2, 1), ("st", 2, 0), ("J5", 2, 2),
+    ("st", 2, 1), ("MX2", 3, 3), ("J5", 2, 3), ("st", 2, 2), ("st", 2, 3), ("J5", 3, 0), ("J5", 3, 1),
+    ("st", 3, 0), ("J5", 3, 2), ("st", 3, 1), ("J5", 3, 3), ("st", 3, 2), ("st", 3, 3),
+]
+
+
+def tile_multiscaleretention_pb_kernel(tc, x, attn, Wg, bg, gn_w, gn_b, Wo, bo, out):
+    nc = tc.nc
+    xf = x.flatten_outer_dims()
+    af = attn.flatten_outer_dims()
+    of = out.flatten_outer_dims()
+
+    with ExitStack() as ctx:
+        const = ctx.enter_context(tc.tile_pool(name="const", bufs=1))
+        rawp = ctx.enter_context(tc.tile_pool(name="rawp", bufs=6))
+        grpp = ctx.enter_context(tc.tile_pool(name="grpp", bufs=5))
+        codep = ctx.enter_context(tc.tile_pool(name="codep", bufs=6))
+        normp = ctx.enter_context(tc.tile_pool(name="normp", bufs=6))
+        gatep = ctx.enter_context(tc.tile_pool(name="gatep", bufs=2))
+        outp = ctx.enter_context(tc.tile_pool(name="outp", bufs=3))
+        psum = ctx.enter_context(tc.psum_pool(name="psum", bufs=4))
+        ctx.enter_context(tc.manual_schedule())
+
+        ident = const.tile([P, P], F32, name="ident")
+        make_identity(nc, ident[:])
+        vraw = const.tile([P, P], BF16, name="vraw")
+        nc.vector.memset(vraw[:], 0.0)
+        eps_t = const.tile([P, 1], F32, name="eps_t")
+        nc.vector.memset(eps_t[:], EPS)
+        nc.scalar.dma_start(out=vraw[0:16, :], in_=bg.rearrange("(r c) -> r c", c=P))
+        nc.scalar.dma_start(out=vraw[16:32, :], in_=gn_w.rearrange("(r c) -> r c", c=P))
+        nc.scalar.dma_start(out=vraw[32:48, :], in_=gn_b.rearrange("(r c) -> r c", c=P))
+        warm = const.tile([P, 1], F32, name="warm")
+        nc.scalar.activation(out=warm[:], in_=eps_t[:], func=ACT.Sqrt, scale=1.0)
+
+        bo_bc = const.tile([P, E], BF16, name="bo_bc")
+        vf = const.tile([P, P], F32, name="vf")
+        vcol = const.tile([P, 48], F32, name="vcol")
+        st = const.tile([P, 64, 6], F32, name="st")
+        dif = const.tile([P, 64], F32, name="dif")
+        mu = const.tile([P, 64], F32, name="mu")
+        m2 = const.tile([P, 64], F32, name="m2")
+        std = const.tile([P, 64], F32, name="std")
+        rstd = const.tile([P, 64], F32, name="rstd")
+        xc = const.tile([P, NPASS, S], U32, name="xc", align_bytes=64)
+        xs = const.tile([P, NPASS, S], U8, name="xs", align_bytes=64)
+        hc = const.tile([P, NPASS, S], U32, name="hc", align_bytes=64)
+        hs = const.tile([P, NPASS, S], U8, name="hs", align_bytes=64)
+        T = {}
+
+        def ld_attn(s):
+            T[("a", s)] = const.tile([P, E], BF16, name="a_sb%d" % s)
+            nc.sync.dma_start(out=T[("a", s)][:], in_=af[P * s:P * s + P, :])
+
+        def ld_raw(kind, a, c):
+            t = rawp.tile([P, 4096], BF16, name="raw_%s%d%d" % (kind, a, c), tag="raw")
+            T[("raw", kind, a, c)] = t
+            if kind == "x":
+                nc.sync.dma_start(
+                    out=t[:].rearrange("p (s k) -> p s k", s=2),
+                    in_=xf[256 * a:256 * a + 256, :].rearrange("(s p) k -> p s k", p=P),
+                )
+            elif kind == "g":
+                tv = t[:].rearrange("p (t c) -> p t c", t=4)
+                for u in range(2):
+                    r0 = 512 * c + 256 * u
+                    nc.sync.dma_start(
+                        out=tv[:, 2 * u:2 * u + 2, :],
+                        in_=Wg[r0:r0 + 256, 1024 * a:1024 * a + 1024].rearrange("(q e) c -> q e c", e=2),
+                    )
+            else:
+                nc.sync.dma_start(
+                    out=t[:].rearrange("p (t c) -> p t c", t=4),
+                    in_=Wo[512 * c:512 * c + 512, 1024 * a:1024 * a + 1024].rearrange("(t p) c -> p t c", p=P),
+                )
+
+        def vec_prep():
+            nc.vector.tensor_copy(out=vf[:], in_=vraw[:])
+            vt = psum.tile([P, P], F32, name="vt", tag="t")
+            nc.tensor.transpose(vt[:], vf[:], ident[:])
+            nc.vector.tensor_copy(out=vcol[:], in_=vt[:, 0:48])
+
+        def bn(s):
+            for g in range(16):
+                nc.vector.bn_stats(out=st[:, 16 * s + g, :], in_=T[("a", s)][:, P * g:P * g + P])
+            if s == 0:
+                vec_prep()
+
+        def small():
+            me, m2e, mo, m2o = st[:, :, 1], st[:, :, 2], st[:, :, 4], st[:, :, 5]
+            nc.vector.tensor_tensor(out=dif[:], in0=me, in1=mo, op=ALU.subtract)
+            nc.vector.tensor_tensor(out=mu[:], in0=me, in1=mo, op=ALU.add)
+            nc.vector.tensor_tensor(out=m2[:], in0=m2e, in1=m2o, op=ALU.add)
+            nc.vector.tensor_tensor(out=dif[:], in0=dif[:], in1=dif[:], op=ALU.mult)
+            nc.vector.tensor_scalar(out=mu[:], in0=mu[:], scalar1=0.5, scalar2=None, op0=ALU.mult)
+            nc.vector.scalar_tensor_tensor(
+                out=m2[:], in0=dif[:], scalar=32.0, in1=m2[:], op0=ALU.mult, op1=ALU.add
+            )
+
+        def x_transpose(g, sp):
+            xt = psum.tile([P, 2, 256], F32, name="xt%d%d" % (g, sp), tag=("z" if sp == 0 else "t"))
+            T[("xt", g, sp)] = xt
+            xw = T[("raw", "x", sp, 0)][:].bitcast(F32)
+            for u in range(2):
+                for sl in range(2):
+                    c0 = 1024 * sl + 256 * g + P * u
+                    nc.tensor.transpose(xt[:, u, P * sl:P * sl + P], xw[:, c0:c0 + P], ident[:])
+
+        def x_evac(g, sp):
+            if ("xq", g) not in T:
+                T[("xq", g)] = grpp.tile([P, 2048], BF16, name="xq%d" % g, tag="grp", align_bytes=64)
+            xq32 = T[("xq", g)][:].bitcast(F32).rearrange("p (r u) -> p r u", u=2)
+            nc.scalar.copy(
+                out=xq32[:, 256 * sp:256 * sp + 256, :], in_=T[("xt", g, sp)][:].rearrange("p u r -> p r u")
+            )
+
+        def regroup(eng, kind, blk, c):
+            raw = T[("raw", kind, blk // 2, c)]
+            col0 = 512 * (blk % 2)
+            src = raw[:].rearrange("p (t c) -> p t c", t=4)[:, :, col0:col0 + 512]
+            g4 = grpp.tile([P, 2048], BF16, name="g4_%s%d%d" % (kind, blk, c), tag="grp", align_bytes=64)
+            T[("g4", kind, blk, c)] = g4
+            dst = g4[:].rearrange("p (c i t) -> p c t i", i=4, t=4)
+            srcv = src.rearrange("p t (c i) -> p c t i", i=4)
+            if eng == "V":
+                nc.vector.tensor_copy(out=dst, in_=srcv)
+            else:
+                nc.scalar.copy(out=dst, in_=srcv)
+
+        def quant(kind, blk, c):
+            if ("wc", kind, blk) not in T:
+                T[("wc", kind, blk)] = codep.tile(
+                    [P, NPASS, 512], U32, name="wc_%s%d" % (kind, blk), tag="wc", align_bytes=64
+                )
+                T[("ws", kind, blk)] = codep.tile(
+                    [P, NPASS, 512], U8, name="ws_%s%d" % (kind, blk), tag="ws", align_bytes=64
+                )
+            nc.vector.quantize_mx(
+                out=T[("wc", kind, blk)][:, c, :].bitcast(FP8X4),
+                scales=T[("ws", kind, blk)][:, c, :],
+                in_=T[("g4", kind, blk, c)][:],
+            )
+
+        def mx1(G, t):
+            z = psum.tile([P, S], F32, name="z%d%d" % (G, t), tag="z")
+            T[("z", G, t)] = z
+            wc, ws = T[("wc", "g", G)], T[("ws", "g", G)]
+            for c in range(NPASS):
+                nc.tensor.matmul_mx(
+                    out=z[:],
+                    lhsT=wc[:, c, P * t:P * t + P].bitcast(FP8X4),
+                    lhsT_scale=ws[:, c, P * t:P * t + P],
+                    rhs=xc[:, c, :].bitcast(FP8X4),
+                    rhs_scale=xs[:, c, :],
+                    start=(c == 0),
+                    stop=(c == NPASS - 1),
+                )
+
+        def normalise(G, s):
+            nrm = normp.tile([P, 512], F32, name="nrm%d%d" % (G, s), tag="nrm")
+            T[("nrm", G, s)] = nrm
+            for t in range(4):
+                gi = 4 * G + t
+                k = 16 * s + gi
+                nc.vector.tensor_scalar(
+                    out=nrm[:, P * t:P * t + P],
+                    in0=T[("a", s)][:, P * gi:P * gi + P],
+                    scalar1=mu[:, k:k + 1],
+                    scalar2=rstd[:, k:k + 1],
+                    op0=ALU.subtract,
+                    op1=ALU.mult,
+                )
+
+        def n_transpose(G, t):
+            nT = psum.tile([P, S], F32, name="nT%d%d" % (G, t), tag="t")
+            T[("nT", G, t)] = nT
+            for s in range(4):
+                nc.tensor.transpose(nT[:, P * s:P * s + P], T[("nrm", G, s)][:, P * t:P * t + P], ident[:])
+
+        def silu(G, t):
+            if ("sil", G) not in T:
+                T[("sil", G)] = gatep.tile([P, 2048], F32, name="sil%d" % G, tag="sil")
+            gi = 4 * G + t
+            nc.scalar.activation(
+                out=T[("sil", G)][:, S * t:S * t + S], in_=T[("z", G, t)][:], func=ACT.Silu,
+                bias=vcol[:, gi:gi + 1], scale=1.0,
+            )
+
+        def gain(G, t):
+            if ("gw", G) not in T:
+                T[("gw", G)] = gatep.tile([P, 2048], F32, name="gw%d" % G, tag="gw")
+            gi = 4 * G + t
+            nc.scalar.activation(
+                out=T[("gw", G)][:, S * t:S * t + S], in_=T[("nT", G, t)][:], func=ACT.Identity,
+                bias=vcol[:, 32 + gi:33 + gi], scale=vcol[:, 16 + gi:17 + gi],
+            )
+
+        def gate_mul(G):
+            hq = grpp.tile([P, 2048], BF16, name="hq%d" % G, tag="grp", align_bytes=64)
+            T[("hq", G)] = hq
+            nc.vector.tensor_tensor(
+                out=hq[:].rearrange("p (c i t) -> p c t i", i=4, t=4),
+                in0=T[("sil", G)][:].rearrange("p (t c i) -> p c t i", t=4, i=4),
+                in1=T[("gw", G)][:].rearrange("p (t c i) -> p c t i", t=4, i=4),
+                op=ALU.mult,
+            )
+
+        def mx2(NB, G):
+            if G == 0:
+                for s in range(4):
+                    T[("acc", NB, s)] = psum.tile(
+                        [P, 512], F32, name="acc%d%d" % (NB, s), tag=("z" if NB % 2 == 0 else "t")
+                    )
+            wc, ws = T[("wc", "o", NB)], T[("ws", "o", NB)]
+            for s in range(4):
+                nc.tensor.matmul_mx(
+                    out=T[("acc", NB, s)][:],
+                    lhsT=hc[:, G, P * s:P * s + P].bitcast(FP8X4),
+                    lhsT_scale=hs[:, G, P * s:P * s + P],
+                    rhs=wc[:, G, :].bitcast(FP8X4),
+                    rhs_scale=ws[:, G, :],
+                    start=(G == 0),
+                    stop=(G == NPASS - 1),
+                )
+
+        def bias_out(NB, s):
+            o_sb = outp.tile([P, 512], F32, name="o%d%d" % (NB, s), tag="o")
+            T[("o", NB, s)] = o_sb
+            nc.vector.tensor_tensor(
+                out=o_sb[:], in0=T[("acc", NB, s)][:], in1=bo_bc[:, 512 * NB:512 * NB + 512], op=ALU.add
+            )
+
+        for tok in ORDER:
+            k = tok[0]
+            if k == "ldA":
+                ld_attn(tok[1])
+            elif k == "ld":
+                ld_raw(tok[1], tok[2], tok[3])
+            elif k == "ldbo":
+                nc.sync.dma_start(out=bo_bc[:], in_=bo.partition_broadcast(P))
+            elif k == "bn":
+                bn(tok[1])
+            elif k == "sm":
+                small()
+            elif k == "sqrt":
+                nc.scalar.activation(out=std[:], in_=m2[:], func=ACT.Sqrt, bias=eps_t[:, 0:1], scale=1.0 / P)
+            elif k == "recip":
+                nc.vector.reciprocal(out=rstd[:], in_=std[:])
+            elif k == "xT":
+                x_transpose(tok[1], tok[2])
+            elif k == "XE":
+                x_evac(tok[1], tok[2])
+            elif k == "Qx":
+                nc.vector.quantize_mx(
+                    out=xc[:, tok[1], :].bitcast(FP8X4), scales=xs[:, tok[1], :], in_=T[("xq", tok[1])][:]
+                )
+            elif k == "RGV":
+                regroup("V", tok[1], tok[2], tok[3])
+            elif k == "RGS":
+                regroup("S", tok[1], tok[2], tok[3])
+            elif k == "Q":
+                quant(tok[1], tok[2], tok[3])
+            elif k == "MX1":
+                mx1(tok[1], tok[2])
+            elif k == "J4":
+                normalise(tok[1], tok[2])
+            elif k == "T":
+                n_transpose(tok[1], tok[2])
+            elif k == "SIL":
+                silu(tok[1], tok[2])
+            elif k == "GW":
+                gain(tok[1], tok[2])
+            elif k == "MUL":
+                gate_mul(tok[1])
+            elif k == "QH":
+                nc.vector.quantize_mx(
+                    out=hc[:, tok[1], :].bitcast(FP8X4), scales=hs[:, tok[1], :], in_=T[("hq", tok[1])][:]
+                )
+            elif k == "MX2":
+                mx2(tok[1], tok[2])
+            elif k == "J5":
+                bias_out(tok[1], tok[2])
+            elif k == "st":
+                NB, s = tok[1], tok[2]
+                nc.sync.dma_start(out=of[P * s:P * s + P, 512 * NB:512 * NB + 512], in_=T[("o", NB, s)][:])
+            else:
+                assert False, k

@@ -19,45 +19,45 @@ NPASS = E // 512
 FLOPS = 2 * 2 * S * E * E
 
 ORDER = [
-    ("ldA", 0), ("ld", "g", 0, 0), ("bn", 0), ("ldA", 1), ("ld", "g", 0, 1), ("RGS", "g", 1, 0),
-    ("RGV", "g", 0, 0), ("bn", 1), ("ldA", 2), ("ld", "g", 0, 2), ("RGS", "g", 0, 1), ("Q", "g", 0, 0),
-    ("Q", "g", 1, 0), ("ldA", 3), ("bn", 2), ("RGS", "g", 1, 1), ("ld", "g", 0, 3), ("Q", "g", 0, 1),
-    ("RGS", "g", 0, 2), ("Q", "g", 1, 1), ("ld", "x", 0, 0), ("bn", 3), ("RGS", "g", 1, 2), ("ld", "x", 1, 0),
-    ("sm",), ("Q", "g", 0, 2), ("sqrt",), ("Q", "g", 1, 2), ("RGS", "g", 0, 3), ("recip",), ("J4", 0, 0),
-    ("xT", 0, 0), ("ld", "g", 1, 0), ("xT", 1, 0), ("J4", 0, 1), ("xT", 2, 0), ("xT", 3, 0), ("J4", 0, 2),
-    ("XE", 0, 0), ("Q", "g", 0, 3), ("XE", 1, 0), ("J4", 0, 3), ("xT", 0, 1), ("XE", 2, 0), ("ld", "g", 1, 1),
-    ("xT", 1, 1), ("XE", 0, 1), ("J4", 1, 0), ("xT", 2, 1), ("xT", 3, 1), ("XE", 1, 1), ("J4", 1, 1),
-    ("T", 0, 0), ("XE", 2, 1), ("T", 0, 1), ("Qx", 0), ("XE", 3, 0), ("T", 0, 2), ("Qx", 1),
-    ("ld", "g", 1, 2), ("XE", 3, 1), ("Qx", 2), ("GW", 0, 0), ("T", 0, 3), ("Qx", 3), ("GW", 0, 1),
-    ("J4", 1, 2), ("GW", 0, 2), ("MX1", 0, 0), ("J4", 1, 3), ("ld", "g", 1, 3), ("GW", 0, 3),
-    ("RGV", "g", 2, 0), ("MX1", 0, 1), ("RGS", "g", 1, 3), ("Q", "g", 2, 0), ("MX1", 0, 2), ("J4", 2, 0),
-    ("ldbo",), ("RGV", "g", 2, 2), ("MX1", 0, 3), ("SIL", 0, 0), ("SIL", 0, 1), ("ld", "o", 0, 0),
-    ("Q", "g", 1, 3), ("T", 1, 0), ("SIL", 0, 2), ("T", 1, 1), ("Q", "g", 2, 2), ("T", 1, 2), ("SIL", 0, 3),
-    ("T", 1, 3), ("RGV", "g", 2, 3), ("MX1", 1, 0), ("GW", 1, 0), ("GW", 1, 1), ("ld", "o", 0, 1), ("MUL", 0),
-    ("MX1", 1, 1), ("GW", 1, 2), ("SIL", 1, 0), ("MX1", 1, 2), ("SIL", 1, 1), ("GW", 1, 3), ("QH", 0),
-    ("MX1", 1, 3), ("SIL", 1, 2), ("Q", "g", 2, 3), ("RGS", "g", 2, 1), ("J4", 2, 1), ("J4", 2, 2),
-    ("J4", 2, 3), ("RGV", "g", 3, 2), ("T", 2, 0), ("SIL", 1, 3), ("T", 2, 1), ("GW", 2, 0), ("T", 2, 2),
-    ("ld", "o", 0, 2), ("MUL", 1), ("T", 2, 3), ("GW", 2, 1), ("GW", 2, 2), ("GW", 2, 3), ("RGS", "g", 3, 0),
-    ("QH", 1), ("Q", "g", 2, 1), ("Q", "g", 3, 2), ("MX1", 2, 0), ("RGV", "g", 3, 3), ("ld", "o", 0, 3),
-    ("RGS", "g", 3, 1), ("MX1", 2, 1), ("Q", "g", 3, 0), ("Q", "g", 3, 3), ("MX1", 2, 2), ("J4", 3, 0),
-    ("SIL", 2, 0), ("ld", "o", 1, 0), ("Q", "g", 3, 1), ("SIL", 2, 1), ("MX1", 2, 3), ("J4", 3, 1),
-    ("SIL", 2, 2), ("J4", 3, 2), ("MX1", 3, 0), ("RGS", "o", 0, 0), ("J4", 3, 3), ("ld", "o", 1, 1),
-    ("MX1", 3, 1), ("RGV", "o", 0, 2), ("SIL", 2, 3), ("T", 3, 0), ("Q", "o", 0, 0), ("T", 3, 1),
-    ("SIL", 3, 0), ("T", 3, 2), ("MUL", 2), ("T", 3, 3), ("GW", 3, 0), ("MX1", 3, 2), ("SIL", 3, 1),
-    ("GW", 3, 1), ("MX1", 3, 3), ("QH", 2), ("SIL", 3, 2), ("Q", "o", 0, 2), ("MX2", 0, 0), ("GW", 3, 2),
-    ("RGV", "o", 1, 2), ("SIL", 3, 3), ("GW", 3, 3), ("ld", "o", 1, 2), ("Q", "o", 1, 2), ("RGS", "o", 0, 1),
-    ("MUL", 3), ("RGS", "o", 0, 3), ("QH", 3), ("Q", "o", 0, 1), ("RGV", "o", 2, 0), ("MX2", 0, 1),
-    ("RGS", "o", 1, 0), ("Q", "o", 0, 3), ("MX2", 0, 2), ("Q", "o", 2, 0), ("RGV", "o", 3, 0), ("MX2", 0, 3),
-    ("ld", "o", 1, 3), ("RGS", "o", 1, 1), ("Q", "o", 1, 0), ("J5", 0, 0), ("MX2", 1, 0), ("J5", 0, 1),
-    ("RGS", "o", 1, 3), ("J5", 0, 2), ("st", 0, 0), ("MX2", 2, 0), ("Q", "o", 1, 1), ("st", 0, 1),
-    ("J5", 0, 3), ("st", 0, 2), ("MX2", 1, 1), ("Q", "o", 3, 0), ("RGS", "o", 2, 1), ("st", 0, 3),
-    ("Q", "o", 1, 3), ("MX2", 1, 2), ("RGV", "o", 3, 1), ("MX2", 1, 3), ("Q", "o", 3, 1), ("RGS", "o", 2, 2),
-    ("Q", "o", 2, 1), ("J5", 1, 0), ("MX2", 2, 1), ("J5", 1, 1), ("st", 1, 0), ("RGS", "o", 2, 3),
-    ("J5", 1, 2), ("st", 1, 1), ("MX2", 3, 0), ("J5", 1, 3), ("st", 1, 2), ("Q", "o", 2, 2), ("st", 1, 3),
-    ("MX2", 3, 1), ("RGV", "o", 3, 3), ("RGS", "o", 3, 2), ("MX2", 2, 2), ("Q", "o", 2, 3), ("Q", "o", 3, 3),
-    ("MX2", 2, 3), ("Q", "o", 3, 2), ("J5", 2, 0), ("MX2", 3, 2), ("J5", 2, 1), ("st", 2, 0), ("J5", 2, 2),
-    ("st", 2, 1), ("MX2", 3, 3), ("J5", 2, 3), ("st", 2, 2), ("st", 2, 3), ("J5", 3, 0), ("J5", 3, 1),
-    ("st", 3, 0), ("J5", 3, 2), ("st", 3, 1), ("J5", 3, 3), ("st", 3, 2), ("st", 3, 3),
+    ("ldA", 0), ("ld", "g", 0, 0), ("ldA", 1), ("bn", 0), ("ld", "g", 0, 1), ("RGS", "g", 0, 0), ("ldA", 2),
+    ("bn", 1), ("ld", "g", 0, 2), ("RGS", "g", 1, 0), ("Q", "g", 0, 0), ("RGV", "g", 1, 1),
+    ("RGS", "g", 0, 1), ("ldA", 3), ("bn", 2), ("ld", "g", 0, 3), ("Q", "g", 0, 1), ("RGV", "g", 0, 2),
+    ("ld", "x", 0, 0), ("bn", 3), ("ld", "x", 1, 0), ("RGS", "g", 0, 3), ("sm",), ("Q", "g", 0, 2),
+    ("Q", "g", 1, 0), ("Q", "g", 1, 1), ("ld", "g", 1, 0), ("sqrt",), ("RGS", "g", 1, 3), ("RGV", "g", 1, 2),
+    ("xT", 0, 0), ("xT", 1, 0), ("recip",), ("Q", "g", 0, 3), ("xT", 2, 0), ("J4", 0, 0), ("xT", 3, 0),
+    ("XE", 0, 0), ("ld", "g", 1, 1), ("J4", 0, 1), ("xT", 0, 1), ("XE", 1, 0), ("J4", 0, 2), ("J4", 0, 3),
+    ("xT", 1, 1), ("XE", 2, 0), ("Q", "g", 1, 2), ("xT", 2, 1), ("XE", 0, 1), ("Q", "g", 1, 3), ("xT", 3, 1),
+    ("XE", 3, 0), ("ld", "g", 1, 2), ("J4", 1, 0), ("T", 0, 0), ("XE", 1, 1), ("Qx", 0), ("XE", 2, 1),
+    ("T", 0, 1), ("J4", 1, 1), ("XE", 3, 1), ("T", 0, 2), ("Qx", 1), ("GW", 0, 0), ("T", 0, 3), ("Qx", 2),
+    ("ld", "g", 1, 3), ("GW", 0, 1), ("Qx", 3), ("GW", 0, 2), ("J4", 1, 2), ("J4", 1, 3), ("GW", 0, 3),
+    ("RGV", "g", 2, 0), ("MX1", 0, 0), ("RGS", "g", 3, 0), ("ldbo",), ("Q", "g", 2, 0), ("MX1", 0, 1),
+    ("RGV", "g", 2, 1), ("ld", "o", 0, 0), ("SIL", 0, 0), ("MX1", 0, 2), ("Q", "g", 2, 1), ("SIL", 0, 1),
+    ("J4", 2, 0), ("RGS", "g", 2, 2), ("MX1", 0, 3), ("J4", 2, 1), ("Q", "g", 3, 0), ("ld", "o", 0, 1),
+    ("RGV", "g", 3, 1), ("T", 1, 0), ("T", 1, 1), ("SIL", 0, 2), ("Q", "g", 3, 1), ("T", 1, 2), ("SIL", 0, 3),
+    ("Q", "g", 2, 2), ("T", 1, 3), ("ld", "o", 0, 2), ("GW", 1, 0), ("RGV", "g", 3, 2), ("MX1", 1, 0),
+    ("GW", 1, 1), ("MUL", 0), ("GW", 1, 2), ("MX1", 1, 1), ("GW", 1, 3), ("SIL", 1, 0), ("ld", "o", 0, 3),
+    ("MX1", 1, 2), ("RGS", "g", 2, 3), ("QH", 0), ("MX1", 1, 3), ("J4", 2, 2), ("J4", 2, 3), ("Q", "g", 3, 2),
+    ("ld", "o", 1, 0), ("SIL", 1, 1), ("T", 2, 0), ("J4", 3, 0), ("SIL", 1, 2), ("Q", "g", 2, 3), ("T", 2, 1),
+    ("J4", 3, 1), ("SIL", 1, 3), ("T", 2, 2), ("RGV", "o", 0, 1), ("GW", 2, 0), ("T", 2, 3), ("MX1", 2, 0),
+    ("GW", 2, 1), ("MUL", 1), ("GW", 2, 2), ("MX1", 2, 1), ("GW", 2, 3), ("SIL", 2, 0), ("MX1", 2, 2),
+    ("RGS", "g", 3, 3), ("QH", 1), ("J4", 3, 2), ("J4", 3, 3), ("MX1", 2, 3), ("Q", "o", 0, 1),
+    ("RGV", "o", 0, 2), ("ld", "o", 1, 1), ("SIL", 2, 1), ("T", 3, 0), ("SIL", 2, 2), ("T", 3, 1),
+    ("Q", "g", 3, 3), ("SIL", 2, 3), ("T", 3, 2), ("Q", "o", 0, 2), ("GW", 3, 0), ("T", 3, 3),
+    ("RGV", "o", 0, 3), ("GW", 3, 1), ("MX1", 3, 0), ("GW", 3, 2), ("MUL", 2), ("GW", 3, 3), ("MX1", 3, 1),
+    ("RGS", "o", 0, 0), ("MX1", 3, 2), ("QH", 2), ("Q", "o", 0, 3), ("MX1", 3, 3), ("SIL", 3, 0),
+    ("RGV", "o", 1, 1), ("SIL", 3, 1), ("SIL", 3, 2), ("ld", "o", 1, 2), ("Q", "o", 0, 0), ("SIL", 3, 3),
+    ("Q", "o", 1, 1), ("RGV", "o", 1, 2), ("RGS", "o", 1, 0), ("MX2", 0, 0), ("MUL", 3), ("ld", "o", 1, 3),
+    ("MX2", 0, 1), ("RGS", "o", 1, 3), ("MX2", 0, 2), ("QH", 3), ("Q", "o", 1, 0), ("RGS", "o", 2, 1),
+    ("Q", "o", 1, 2), ("MX2", 0, 3), ("Q", "o", 1, 3), ("RGV", "o", 2, 0), ("MX2", 1, 0), ("RGS", "o", 2, 2),
+    ("J5", 0, 0), ("MX2", 1, 1), ("J5", 0, 1), ("st", 0, 0), ("J5", 0, 2), ("Q", "o", 2, 0), ("st", 0, 1),
+    ("MX2", 1, 2), ("RGS", "o", 3, 0), ("J5", 0, 3), ("st", 0, 2), ("Q", "o", 2, 1), ("MX2", 1, 3),
+    ("st", 0, 3), ("Q", "o", 2, 2), ("RGV", "o", 2, 3), ("RGS", "o", 3, 1), ("MX2", 2, 0), ("Q", "o", 2, 3),
+    ("MX2", 2, 1), ("J5", 1, 0), ("J5", 1, 1), ("RGS", "o", 3, 3), ("MX2", 2, 2), ("st", 1, 0), ("J5", 1, 2),
+    ("Q", "o", 3, 0), ("st", 1, 1), ("MX2", 2, 3), ("J5", 1, 3), ("st", 1, 2), ("Q", "o", 3, 1), ("st", 1, 3),
+    ("RGV", "o", 3, 2), ("MX2", 3, 0), ("Q", "o", 3, 2), ("MX2", 3, 1), ("Q", "o", 3, 3), ("J5", 2, 0),
+    ("MX2", 3, 2), ("J5", 2, 1), ("st", 2, 0), ("J5", 2, 2), ("MX2", 3, 3), ("st", 2, 1), ("J5", 2, 3),
+    ("st", 2, 2), ("st", 2, 3), ("J5", 3, 0), ("J5", 3, 1), ("st", 3, 0), ("J5", 3, 2), ("st", 3, 1),
+    ("J5", 3, 3), ("st", 3, 2), ("st", 3, 3),
 ]
 
 
@@ -75,8 +75,8 @@ def tile_multiscaleretention_pb_kernel(tc, x, attn, Wg, bg, gn_w, gn_b, Wo, bo, 
         normp = ctx.enter_context(tc.tile_pool(name="normp", bufs=6))
         gatep = ctx.enter_context(tc.tile_pool(name="gatep", bufs=2))
         outp = ctx.enter_context(tc.tile_pool(name="outp", bufs=3))
-        psum = ctx.enter_context(tc.psum_pool(name="psum", bufs=4))
-        ctx.enter_context(tc.manual_schedule())
+        psum = ctx.enter_context(tc.psum_pool(name="psum", bufs=8))
+
 
         ident = const.tile([P, P], F32, name="ident")
         make_identity(nc, ident[:])
@@ -133,7 +133,7 @@ def tile_multiscaleretention_pb_kernel(tc, x, attn, Wg, bg, gn_w, gn_b, Wo, bo, 
 
         def vec_prep():
             nc.vector.tensor_copy(out=vf[:], in_=vraw[:])
-            vt = psum.tile([P, P], F32, name="vt", tag="t")
+            vt = psum.tile([P, P], F32, name="vt", tag="ps")
             nc.tensor.transpose(vt[:], vf[:], ident[:])
             nc.vector.tensor_copy(out=vcol[:], in_=vt[:, 0:48])
 
@@ -155,7 +155,7 @@ def tile_multiscaleretention_pb_kernel(tc, x, attn, Wg, bg, gn_w, gn_b, Wo, bo, 
             )
 
         def x_transpose(g, sp):
-            xt = psum.tile([P, 2, 256], F32, name="xt%d%d" % (g, sp), tag=("z" if sp == 0 else "t"))
+            xt = psum.tile([P, 2, 256], F32, name="xt%d%d" % (g, sp), tag="ps")
             T[("xt", g, sp)] = xt
             xw = T[("raw", "x", sp, 0)][:].bitcast(F32)
             for u in range(2):
@@ -199,7 +199,7 @@ def tile_multiscaleretention_pb_kernel(tc, x, attn, Wg, bg, gn_w, gn_b, Wo, bo, 
             )
 
         def mx1(G, t):
-            z = psum.tile([P, S], F32, name="z%d%d" % (G, t), tag="z")
+            z = psum.tile([P, S], F32, name="z%d%d" % (G, t), tag="ps")
             T[("z", G, t)] = z
             wc, ws = T[("wc", "g", G)], T[("ws", "g", G)]
             for c in range(NPASS):
@@ -229,7 +229,7 @@ def tile_multiscaleretention_pb_kernel(tc, x, attn, Wg, bg, gn_w, gn_b, Wo, bo, 
                 )
 
         def n_transpose(G, t):
-            nT = psum.tile([P, S], F32, name="nT%d%d" % (G, t), tag="t")
+            nT = psum.tile([P, S], F32, name="nT%d%d" % (G, t), tag="ps")
             T[("nT", G, t)] = nT
             for s in range(4):
                 nc.tensor.transpose(nT[:, P * s:P * s + P], T[("nrm", G, s)][:, P * t:P * t + P], ident[:])
@@ -266,7 +266,7 @@ def tile_multiscaleretention_pb_kernel(tc, x, attn, Wg, bg, gn_w, gn_b, Wo, bo, 
             if G == 0:
                 for s in range(4):
                     T[("acc", NB, s)] = psum.tile(
-                        [P, 512], F32, name="acc%d%d" % (NB, s), tag=("z" if NB % 2 == 0 else "t")
+                        [P, 512], F32, name="acc%d%d" % (NB, s), tag="ps"
                     )
             wc, ws = T[("wc", "o", NB)], T[("ws", "o", NB)]
             for s in range(4):

@@ -19,45 +19,45 @@ NPASS = E // 512
 FLOPS = 2 * 2 * S * E * E
 
 ORDER = [
-    ("ldA", 0), ("ld", "g", 0, 0), ("ldA", 1), ("bn", 0), ("ld", "g", 0, 1), ("RGS", "g", 0, 0), ("ldA", 2),
-    ("bn", 1), ("ld", "g", 0, 2), ("RGS", "g", 1, 0), ("Q", "g", 0, 0), ("RGV", "g", 1, 1),
-    ("RGS", "g", 0, 1), ("ldA", 3), ("bn", 2), ("ld", "g", 0, 3), ("Q", "g", 0, 1), ("RGV", "g", 0, 2),
-    ("ld", "x", 0, 0), ("bn", 3), ("ld", "x", 1, 0), ("RGS", "g", 0, 3), ("sm",), ("Q", "g", 0, 2),
-    ("Q", "g", 1, 0), ("Q", "g", 1, 1), ("ld", "g", 1, 0), ("sqrt",), ("RGS", "g", 1, 3), ("RGV", "g", 1, 2),
-    ("xT", 0, 0), ("xT", 1, 0), ("recip",), ("Q", "g", 0, 3), ("xT", 2, 0), ("J4", 0, 0), ("xT", 3, 0),
-    ("XE", 0, 0), ("ld", "g", 1, 1), ("J4", 0, 1), ("xT", 0, 1), ("XE", 1, 0), ("J4", 0, 2), ("J4", 0, 3),
-    ("xT", 1, 1), ("XE", 2, 0), ("Q", "g", 1, 2), ("xT", 2, 1), ("XE", 0, 1), ("Q", "g", 1, 3), ("xT", 3, 1),
-    ("XE", 3, 0), ("ld", "g", 1, 2), ("J4", 1, 0), ("T", 0, 0), ("XE", 1, 1), ("Qx", 0), ("XE", 2, 1),
-    ("T", 0, 1), ("J4", 1, 1), ("XE", 3, 1), ("T", 0, 2), ("Qx", 1), ("GW", 0, 0), ("T", 0, 3), ("Qx", 2),
-    ("ld", "g", 1, 3), ("GW", 0, 1), ("Qx", 3), ("GW", 0, 2), ("J4", 1, 2), ("J4", 1, 3), ("GW", 0, 3),
-    ("RGV", "g", 2, 0), ("MX1", 0, 0), ("RGS", "g", 3, 0), ("ldbo",), ("Q", "g", 2, 0), ("MX1", 0, 1),
-    ("RGV", "g", 2, 1), ("ld", "o", 0, 0), ("SIL", 0, 0), ("MX1", 0, 2), ("Q", "g", 2, 1), ("SIL", 0, 1),
-    ("J4", 2, 0), ("RGS", "g", 2, 2), ("MX1", 0, 3), ("J4", 2, 1), ("Q", "g", 3, 0), ("ld", "o", 0, 1),
-    ("RGV", "g", 3, 1), ("T", 1, 0), ("T", 1, 1), ("SIL", 0, 2), ("Q", "g", 3, 1), ("T", 1, 2), ("SIL", 0, 3),
-    ("Q", "g", 2, 2), ("T", 1, 3), ("ld", "o", 0, 2), ("GW", 1, 0), ("RGV", "g", 3, 2), ("MX1", 1, 0),
-    ("GW", 1, 1), ("MUL", 0), ("GW", 1, 2), ("MX1", 1, 1), ("GW", 1, 3), ("SIL", 1, 0), ("ld", "o", 0, 3),
-    ("MX1", 1, 2), ("RGS", "g", 2, 3), ("QH", 0), ("MX1", 1, 3), ("J4", 2, 2), ("J4", 2, 3), ("Q", "g", 3, 2),
-    ("ld", "o", 1, 0), ("SIL", 1, 1), ("T", 2, 0), ("J4", 3, 0), ("SIL", 1, 2), ("Q", "g", 2, 3), ("T", 2, 1),
-    ("J4", 3, 1), ("SIL", 1, 3), ("T", 2, 2), ("RGV", "o", 0, 1), ("GW", 2, 0), ("T", 2, 3), ("MX1", 2, 0),
-    ("GW", 2, 1), ("MUL", 1), ("GW", 2, 2), ("MX1", 2, 1), ("GW", 2, 3), ("SIL", 2, 0), ("MX1", 2, 2),
-    ("RGS", "g", 3, 3), ("QH", 1), ("J4", 3, 2), ("J4", 3, 3), ("MX1", 2, 3), ("Q", "o", 0, 1),
-    ("RGV", "o", 0, 2), ("ld", "o", 1, 1), ("SIL", 2, 1), ("T", 3, 0), ("SIL", 2, 2), ("T", 3, 1),
-    ("Q", "g", 3, 3), ("SIL", 2, 3), ("T", 3, 2), ("Q", "o", 0, 2), ("GW", 3, 0), ("T", 3, 3),
-    ("RGV", "o", 0, 3), ("GW", 3, 1), ("MX1", 3, 0), ("GW", 3, 2), ("MUL", 2), ("GW", 3, 3), ("MX1", 3, 1),
-    ("RGS", "o", 0, 0), ("MX1", 3, 2), ("QH", 2), ("Q", "o", 0, 3), ("MX1", 3, 3), ("SIL", 3, 0),
-    ("RGV", "o", 1, 1), ("SIL", 3, 1), ("SIL", 3, 2), ("ld", "o", 1, 2), ("Q", "o", 0, 0), ("SIL", 3, 3),
-    ("Q", "o", 1, 1), ("RGV", "o", 1, 2), ("RGS", "o", 1, 0), ("MX2", 0, 0), ("MUL", 3), ("ld", "o", 1, 3),
-    ("MX2", 0, 1), ("RGS", "o", 1, 3), ("MX2", 0, 2), ("QH", 3), ("Q", "o", 1, 0), ("RGS", "o", 2, 1),
-    ("Q", "o", 1, 2), ("MX2", 0, 3), ("Q", "o", 1, 3), ("RGV", "o", 2, 0), ("MX2", 1, 0), ("RGS", "o", 2, 2),
-    ("J5", 0, 0), ("MX2", 1, 1), ("J5", 0, 1), ("st", 0, 0), ("J5", 0, 2), ("Q", "o", 2, 0), ("st", 0, 1),
-    ("MX2", 1, 2), ("RGS", "o", 3, 0), ("J5", 0, 3), ("st", 0, 2), ("Q", "o", 2, 1), ("MX2", 1, 3),
-    ("st", 0, 3), ("Q", "o", 2, 2), ("RGV", "o", 2, 3), ("RGS", "o", 3, 1), ("MX2", 2, 0), ("Q", "o", 2, 3),
-    ("MX2", 2, 1), ("J5", 1, 0), ("J5", 1, 1), ("RGS", "o", 3, 3), ("MX2", 2, 2), ("st", 1, 0), ("J5", 1, 2),
-    ("Q", "o", 3, 0), ("st", 1, 1), ("MX2", 2, 3), ("J5", 1, 3), ("st", 1, 2), ("Q", "o", 3, 1), ("st", 1, 3),
-    ("RGV", "o", 3, 2), ("MX2", 3, 0), ("Q", "o", 3, 2), ("MX2", 3, 1), ("Q", "o", 3, 3), ("J5", 2, 0),
-    ("MX2", 3, 2), ("J5", 2, 1), ("st", 2, 0), ("J5", 2, 2), ("MX2", 3, 3), ("st", 2, 1), ("J5", 2, 3),
-    ("st", 2, 2), ("st", 2, 3), ("J5", 3, 0), ("J5", 3, 1), ("st", 3, 0), ("J5", 3, 2), ("st", 3, 1),
-    ("J5", 3, 3), ("st", 3, 2), ("st", 3, 3),
+    ("ldA", 0), ("ld", "g", 0, 0), ("ldA", 1), ("bn", 0), ("ld", "g", 0, 1), ("RGV", "g", 0, 0),
+    ("RGS", "g", 1, 0), ("ldA", 2), ("bn", 1), ("ld", "g", 0, 2), ("Q", "g", 0, 0), ("RGS", "g", 0, 1),
+    ("Q", "g", 1, 0), ("ldA", 3), ("bn", 2), ("ld", "g", 0, 3), ("RGS", "g", 1, 1), ("Q", "g", 0, 1),
+    ("RGV", "g", 0, 2), ("RGS", "g", 1, 2), ("ld", "x", 0, 0), ("bn", 3), ("ld", "x", 1, 0),
+    ("RGS", "g", 0, 3), ("sm",), ("Q", "g", 0, 2), ("Q", "g", 1, 1), ("ld", "g", 1, 0), ("sqrt",),
+    ("Q", "g", 1, 2), ("xT", 0, 0), ("recip",), ("xT", 1, 0), ("Q", "g", 0, 3), ("XE", 0, 0), ("xT", 2, 0),
+    ("J4", 0, 0), ("XE", 1, 0), ("J4", 0, 1), ("xT", 3, 0), ("ld", "g", 1, 1), ("J4", 0, 2), ("XE", 2, 0),
+    ("xT", 0, 1), ("J4", 0, 3), ("XE", 3, 0), ("xT", 1, 1), ("RGV", "g", 1, 3), ("XE", 0, 1), ("xT", 2, 1),
+    ("XE", 1, 1), ("xT", 3, 1), ("Q", "g", 1, 3), ("ld", "g", 1, 2), ("XE", 2, 1), ("T", 0, 0), ("Qx", 0),
+    ("XE", 3, 1), ("T", 0, 1), ("Qx", 1), ("GW", 0, 0), ("T", 0, 2), ("Qx", 2), ("GW", 0, 1), ("T", 0, 3),
+    ("Qx", 3), ("ld", "g", 1, 3), ("GW", 0, 2), ("J4", 1, 0), ("GW", 0, 3), ("J4", 1, 1), ("RGS", "g", 2, 1),
+    ("MX1", 0, 0), ("J4", 1, 2), ("J4", 1, 3), ("RGV", "g", 2, 0), ("ldbo",), ("MX1", 0, 1), ("SIL", 0, 0),
+    ("Q", "g", 2, 0), ("ld", "o", 0, 0), ("MX1", 0, 2), ("RGS", "g", 3, 1), ("Q", "g", 2, 1),
+    ("RGV", "g", 2, 2), ("MX1", 0, 3), ("Q", "g", 2, 2), ("ld", "o", 0, 1), ("SIL", 0, 1), ("T", 1, 0),
+    ("J4", 2, 0), ("SIL", 0, 2), ("T", 1, 1), ("J4", 2, 1), ("T", 1, 2), ("SIL", 0, 3), ("RGV", "g", 3, 0),
+    ("T", 1, 3), ("GW", 1, 0), ("MX1", 1, 0), ("ld", "o", 0, 2), ("GW", 1, 1), ("MUL", 0), ("GW", 1, 2),
+    ("MX1", 1, 1), ("GW", 1, 3), ("SIL", 1, 0), ("MX1", 1, 2), ("RGS", "g", 2, 3), ("ld", "o", 0, 3),
+    ("QH", 0), ("J4", 2, 2), ("MX1", 1, 3), ("J4", 2, 3), ("Q", "g", 3, 0), ("SIL", 1, 1), ("Q", "g", 3, 1),
+    ("T", 2, 0), ("SIL", 1, 2), ("Q", "g", 2, 3), ("T", 2, 1), ("SIL", 1, 3), ("T", 2, 2), ("RGV", "g", 3, 2),
+    ("GW", 2, 0), ("T", 2, 3), ("GW", 2, 1), ("MX1", 2, 0), ("ld", "o", 1, 0), ("MUL", 1), ("GW", 2, 2),
+    ("GW", 2, 3), ("MX1", 2, 1), ("SIL", 2, 0), ("RGS", "g", 3, 3), ("QH", 1), ("MX1", 2, 2),
+    ("Q", "g", 3, 2), ("J4", 3, 0), ("MX1", 2, 3), ("J4", 3, 1), ("ld", "o", 1, 1), ("SIL", 2, 1),
+    ("J4", 3, 2), ("Q", "g", 3, 3), ("SIL", 2, 2), ("SIL", 2, 3), ("J4", 3, 3), ("RGV", "o", 0, 2),
+    ("RGS", "o", 0, 0), ("MX1", 3, 0), ("MUL", 2), ("T", 3, 0), ("T", 3, 1), ("SIL", 3, 0), ("T", 3, 2),
+    ("GW", 3, 0), ("T", 3, 3), ("GW", 3, 1), ("QH", 2), ("MX1", 3, 1), ("GW", 3, 2), ("Q", "o", 0, 0),
+    ("GW", 3, 3), ("Q", "o", 0, 2), ("MX1", 3, 2), ("RGS", "o", 0, 1), ("RGV", "o", 0, 3), ("MX1", 3, 3),
+    ("Q", "o", 0, 3), ("RGV", "o", 1, 0), ("SIL", 3, 1), ("MX2", 0, 0), ("SIL", 3, 2), ("ld", "o", 1, 2),
+    ("Q", "o", 0, 1), ("SIL", 3, 3), ("Q", "o", 1, 0), ("RGS", "o", 1, 1), ("RGV", "o", 2, 0), ("MX2", 0, 1),
+    ("MUL", 3), ("MX2", 0, 2), ("ld", "o", 1, 3), ("RGS", "o", 1, 2), ("MX2", 1, 0), ("QH", 3),
+    ("RGS", "o", 1, 3), ("Q", "o", 1, 1), ("Q", "o", 1, 2), ("MX2", 0, 3), ("Q", "o", 2, 0),
+    ("RGV", "o", 2, 1), ("RGS", "o", 2, 2), ("MX2", 1, 1), ("Q", "o", 1, 3), ("MX2", 1, 2), ("J5", 0, 0),
+    ("RGS", "o", 2, 3), ("J5", 0, 1), ("MX2", 1, 3), ("st", 0, 0), ("J5", 0, 2), ("st", 0, 1), ("J5", 0, 3),
+    ("st", 0, 2), ("Q", "o", 2, 1), ("MX2", 2, 0), ("RGS", "o", 3, 0), ("st", 0, 3), ("Q", "o", 2, 2),
+    ("Q", "o", 2, 3), ("MX2", 2, 1), ("J5", 1, 0), ("RGS", "o", 3, 1), ("J5", 1, 1), ("MX2", 2, 2),
+    ("st", 1, 0), ("J5", 1, 2), ("st", 1, 1), ("J5", 1, 3), ("MX2", 2, 3), ("st", 1, 2), ("RGS", "o", 3, 3),
+    ("Q", "o", 3, 0), ("st", 1, 3), ("Q", "o", 3, 1), ("RGV", "o", 3, 2), ("MX2", 3, 0), ("Q", "o", 3, 2),
+    ("MX2", 3, 1), ("Q", "o", 3, 3), ("J5", 2, 0), ("MX2", 3, 2), ("J5", 2, 1), ("st", 2, 0), ("J5", 2, 2),
+    ("MX2", 3, 3), ("st", 2, 1), ("J5", 2, 3), ("st", 2, 2), ("st", 2, 3), ("J5", 3, 0), ("J5", 3, 1),
+    ("st", 3, 0), ("J5", 3, 2), ("st", 3, 1), ("J5", 3, 3), ("st", 3, 2), ("st", 3, 3),
 ]
 
 
@@ -107,7 +107,10 @@ def tile_multiscaleretention_pb_kernel(tc, x, attn, Wg, bg, gn_w, gn_b, Wo, bo, 
 
         def ld_attn(s):
             T[("a", s)] = const.tile([P, E], BF16, name="a_sb%d" % s)
-            nc.sync.dma_start(out=T[("a", s)][:], in_=af[P * s:P * s + P, :])
+            cuts = 2 if s == 0 else 1
+            w = E // cuts
+            for i in range(cuts):
+                nc.sync.dma_start(out=T[("a", s)][:, w * i:w * i + w], in_=af[P * s:P * s + P, w * i:w * i + w])
 
         def ld_raw(kind, a, c):
             t = rawp.tile([P, 4096], BF16, name="raw_%s%d%d" % (kind, a, c), tag="raw")
@@ -119,12 +122,16 @@ def tile_multiscaleretention_pb_kernel(tc, x, attn, Wg, bg, gn_w, gn_b, Wo, bo, 
                 )
             elif kind == "g":
                 tv = t[:].rearrange("p (t c) -> p t c", t=4)
-                for u in range(2):
-                    r0 = 512 * c + 256 * u
-                    nc.sync.dma_start(
-                        out=tv[:, 2 * u:2 * u + 2, :],
-                        in_=Wg[r0:r0 + 256, 1024 * a:1024 * a + 1024].rearrange("(q e) c -> q e c", e=2),
-                    )
+                cuts = 2 if (a == 0 and c == 0) else 1
+                w = 1024 // cuts
+                for i in range(cuts):
+                    for u in range(2):
+                        r0 = 512 * c + 256 * u
+                        c0 = 1024 * a + w * i
+                        nc.sync.dma_start(
+                            out=tv[:, 2 * u:2 * u + 2, w * i:w * i + w],
+                            in_=Wg[r0:r0 + 256, c0:c0 + w].rearrange("(q e) c -> q e c", e=2),
+                        )
             else:
                 nc.sync.dma_start(
                     out=t[:].rearrange("p (t c) -> p t c", t=4),

@@ -19,45 +19,46 @@ NPASS = E // 512
 FLOPS = 2 * 2 * S * E * E
 
 ORDER = [
-    ("ldA", 0), ("ld", "g", 0, 0), ("ldA", 1), ("bn", 0), ("ld", "g", 0, 1), ("RGV", "g", 0, 0),
-    ("RGS", "g", 1, 0), ("ldA", 2), ("bn", 1), ("ld", "g", 0, 2), ("Q", "g", 0, 0), ("RGS", "g", 0, 1),
-    ("Q", "g", 1, 0), ("ldA", 3), ("bn", 2), ("ld", "g", 0, 3), ("RGS", "g", 1, 1), ("Q", "g", 0, 1),
-    ("RGV", "g", 0, 2), ("RGS", "g", 1, 2), ("ld", "x", 0, 0), ("bn", 3), ("ld", "x", 1, 0),
-    ("RGS", "g", 0, 3), ("sm",), ("Q", "g", 0, 2), ("Q", "g", 1, 1), ("ld", "g", 1, 0), ("sqrt",),
-    ("Q", "g", 1, 2), ("xT", 0, 0), ("recip",), ("xT", 1, 0), ("Q", "g", 0, 3), ("XE", 0, 0), ("xT", 2, 0),
-    ("J4", 0, 0), ("XE", 1, 0), ("J4", 0, 1), ("xT", 3, 0), ("ld", "g", 1, 1), ("J4", 0, 2), ("XE", 2, 0),
-    ("xT", 0, 1), ("J4", 0, 3), ("XE", 3, 0), ("xT", 1, 1), ("RGV", "g", 1, 3), ("XE", 0, 1), ("xT", 2, 1),
-    ("XE", 1, 1), ("xT", 3, 1), ("Q", "g", 1, 3), ("ld", "g", 1, 2), ("XE", 2, 1), ("T", 0, 0), ("Qx", 0),
-    ("XE", 3, 1), ("T", 0, 1), ("Qx", 1), ("GW", 0, 0), ("T", 0, 2), ("Qx", 2), ("GW", 0, 1), ("T", 0, 3),
-    ("Qx", 3), ("ld", "g", 1, 3), ("GW", 0, 2), ("J4", 1, 0), ("GW", 0, 3), ("J4", 1, 1), ("RGS", "g", 2, 1),
-    ("MX1", 0, 0), ("J4", 1, 2), ("J4", 1, 3), ("RGV", "g", 2, 0), ("ldbo",), ("MX1", 0, 1), ("SIL", 0, 0),
-    ("Q", "g", 2, 0), ("ld", "o", 0, 0), ("MX1", 0, 2), ("RGS", "g", 3, 1), ("Q", "g", 2, 1),
-    ("RGV", "g", 2, 2), ("MX1", 0, 3), ("Q", "g", 2, 2), ("ld", "o", 0, 1), ("SIL", 0, 1), ("T", 1, 0),
-    ("J4", 2, 0), ("SIL", 0, 2), ("T", 1, 1), ("J4", 2, 1), ("T", 1, 2), ("SIL", 0, 3), ("RGV", "g", 3, 0),
-    ("T", 1, 3), ("GW", 1, 0), ("MX1", 1, 0), ("ld", "o", 0, 2), ("GW", 1, 1), ("MUL", 0), ("GW", 1, 2),
-    ("MX1", 1, 1), ("GW", 1, 3), ("SIL", 1, 0), ("MX1", 1, 2), ("RGS", "g", 2, 3), ("ld", "o", 0, 3),
-    ("QH", 0), ("J4", 2, 2), ("MX1", 1, 3), ("J4", 2, 3), ("Q", "g", 3, 0), ("SIL", 1, 1), ("Q", "g", 3, 1),
-    ("T", 2, 0), ("SIL", 1, 2), ("Q", "g", 2, 3), ("T", 2, 1), ("SIL", 1, 3), ("T", 2, 2), ("RGV", "g", 3, 2),
-    ("GW", 2, 0), ("T", 2, 3), ("GW", 2, 1), ("MX1", 2, 0), ("ld", "o", 1, 0), ("MUL", 1), ("GW", 2, 2),
-    ("GW", 2, 3), ("MX1", 2, 1), ("SIL", 2, 0), ("RGS", "g", 3, 3), ("QH", 1), ("MX1", 2, 2),
-    ("Q", "g", 3, 2), ("J4", 3, 0), ("MX1", 2, 3), ("J4", 3, 1), ("ld", "o", 1, 1), ("SIL", 2, 1),
-    ("J4", 3, 2), ("Q", "g", 3, 3), ("SIL", 2, 2), ("SIL", 2, 3), ("J4", 3, 3), ("RGV", "o", 0, 2),
-    ("RGS", "o", 0, 0), ("MX1", 3, 0), ("MUL", 2), ("T", 3, 0), ("T", 3, 1), ("SIL", 3, 0), ("T", 3, 2),
-    ("GW", 3, 0), ("T", 3, 3), ("GW", 3, 1), ("QH", 2), ("MX1", 3, 1), ("GW", 3, 2), ("Q", "o", 0, 0),
-    ("GW", 3, 3), ("Q", "o", 0, 2), ("MX1", 3, 2), ("RGS", "o", 0, 1), ("RGV", "o", 0, 3), ("MX1", 3, 3),
-    ("Q", "o", 0, 3), ("RGV", "o", 1, 0), ("SIL", 3, 1), ("MX2", 0, 0), ("SIL", 3, 2), ("ld", "o", 1, 2),
-    ("Q", "o", 0, 1), ("SIL", 3, 3), ("Q", "o", 1, 0), ("RGS", "o", 1, 1), ("RGV", "o", 2, 0), ("MX2", 0, 1),
-    ("MUL", 3), ("MX2", 0, 2), ("ld", "o", 1, 3), ("RGS", "o", 1, 2), ("MX2", 1, 0), ("QH", 3),
-    ("RGS", "o", 1, 3), ("Q", "o", 1, 1), ("Q", "o", 1, 2), ("MX2", 0, 3), ("Q", "o", 2, 0),
-    ("RGV", "o", 2, 1), ("RGS", "o", 2, 2), ("MX2", 1, 1), ("Q", "o", 1, 3), ("MX2", 1, 2), ("J5", 0, 0),
-    ("RGS", "o", 2, 3), ("J5", 0, 1), ("MX2", 1, 3), ("st", 0, 0), ("J5", 0, 2), ("st", 0, 1), ("J5", 0, 3),
-    ("st", 0, 2), ("Q", "o", 2, 1), ("MX2", 2, 0), ("RGS", "o", 3, 0), ("st", 0, 3), ("Q", "o", 2, 2),
-    ("Q", "o", 2, 3), ("MX2", 2, 1), ("J5", 1, 0), ("RGS", "o", 3, 1), ("J5", 1, 1), ("MX2", 2, 2),
-    ("st", 1, 0), ("J5", 1, 2), ("st", 1, 1), ("J5", 1, 3), ("MX2", 2, 3), ("st", 1, 2), ("RGS", "o", 3, 3),
-    ("Q", "o", 3, 0), ("st", 1, 3), ("Q", "o", 3, 1), ("RGV", "o", 3, 2), ("MX2", 3, 0), ("Q", "o", 3, 2),
-    ("MX2", 3, 1), ("Q", "o", 3, 3), ("J5", 2, 0), ("MX2", 3, 2), ("J5", 2, 1), ("st", 2, 0), ("J5", 2, 2),
-    ("MX2", 3, 3), ("st", 2, 1), ("J5", 2, 3), ("st", 2, 2), ("st", 2, 3), ("J5", 3, 0), ("J5", 3, 1),
-    ("st", 3, 0), ("J5", 3, 2), ("st", 3, 1), ("J5", 3, 3), ("st", 3, 2), ("st", 3, 3),
+    ("ldA", 0), ("ld", "g", 0, 0), ("ldA", 1), ("bn", 0), ("ld", "g", 0, 1), ("RGS", "g", 0, 0),
+    ("RGV", "g", 1, 0), ("ldA", 2), ("Q", "g", 1, 0), ("bn", 1), ("ld", "g", 0, 2), ("RGS", "g", 0, 1),
+    ("Q", "g", 0, 0), ("ldA", 3), ("bn", 2), ("ld", "g", 0, 3), ("RGS", "g", 1, 1), ("Q", "g", 0, 1),
+    ("RGV", "g", 0, 2), ("RGS", "g", 1, 2), ("ld", "x", 0, 0), ("bn", 3), ("ld", "x", 1, 0), ("sm",),
+    ("RGS", "g", 0, 3), ("Q", "g", 0, 2), ("Q", "g", 1, 1), ("Q", "g", 1, 2), ("ld", "g", 1, 0), ("sqrt",),
+    ("RGV", "g", 1, 3), ("xT", 0, 0), ("xT", 1, 0), ("recip",), ("Q", "g", 0, 3), ("XE", 0, 0), ("xT", 2, 0),
+    ("J4", 0, 0), ("XE", 1, 0), ("xT", 3, 0), ("J4", 0, 1), ("ld", "g", 1, 1), ("XE", 2, 0), ("J4", 0, 2),
+    ("xT", 0, 1), ("J4", 0, 3), ("XE", 3, 0), ("xT", 1, 1), ("Q", "g", 1, 3), ("XE", 0, 1), ("xT", 2, 1),
+    ("J4", 1, 0), ("XE", 1, 1), ("xT", 3, 1), ("J4", 1, 1), ("ld", "g", 1, 2), ("Qx", 0), ("XE", 2, 1),
+    ("T", 0, 0), ("Qx", 1), ("XE", 3, 1), ("T", 0, 1), ("Qx", 2), ("GW", 0, 0), ("T", 0, 2), ("Qx", 3),
+    ("GW", 0, 1), ("T", 0, 3), ("RGV", "g", 2, 0), ("ld", "g", 1, 3), ("GW", 0, 2), ("GW", 0, 3),
+    ("MX1", 0, 0), ("J4", 1, 2), ("RGS", "g", 2, 1), ("J4", 1, 3), ("Q", "g", 2, 0), ("MX1", 0, 1),
+    ("J4", 2, 0), ("ldbo",), ("RGV", "g", 2, 2), ("MX1", 0, 2), ("SIL", 0, 0), ("ld", "o", 0, 0),
+    ("Q", "g", 2, 1), ("SIL", 0, 1), ("MX1", 0, 3), ("Q", "g", 2, 2), ("RGS", "g", 3, 1), ("J4", 2, 1),
+    ("RGV", "g", 3, 0), ("T", 1, 0), ("ld", "o", 0, 1), ("T", 1, 1), ("Q", "g", 3, 0), ("SIL", 0, 2),
+    ("T", 1, 2), ("RGV", "g", 3, 2), ("SIL", 0, 3), ("T", 1, 3), ("GW", 1, 0), ("MX1", 1, 0),
+    ("Q", "g", 3, 1), ("ld", "o", 0, 2), ("GW", 1, 1), ("MUL", 0), ("GW", 1, 2), ("MX1", 1, 1), ("GW", 1, 3),
+    ("SIL", 1, 0), ("MX1", 1, 2), ("SIL", 1, 1), ("ld", "o", 0, 3), ("QH", 0), ("RGS", "g", 2, 3),
+    ("MX1", 1, 3), ("J4", 2, 2), ("J4", 2, 3), ("Q", "g", 3, 2), ("T", 2, 0), ("RGV", "g", 3, 3),
+    ("ld", "o", 1, 0), ("T", 2, 1), ("SIL", 1, 2), ("Q", "g", 3, 3), ("T", 2, 2), ("SIL", 1, 3),
+    ("Q", "g", 2, 3), ("T", 2, 3), ("GW", 2, 0), ("J4", 3, 0), ("GW", 2, 1), ("MX1", 3, 0), ("MUL", 1),
+    ("ld", "o", 1, 1), ("GW", 2, 2), ("GW", 2, 3), ("MX1", 2, 0), ("SIL", 3, 0), ("QH", 1),
+    ("RGS", "o", 0, 2), ("MX1", 2, 1), ("J4", 3, 1), ("J4", 3, 2), ("MX1", 2, 2), ("J4", 3, 3),
+    ("RGV", "o", 0, 0), ("SIL", 2, 0), ("MX1", 2, 3), ("SIL", 2, 1), ("Q", "o", 0, 0), ("SIL", 2, 2),
+    ("RGV", "o", 0, 1), ("T", 3, 0), ("RGS", "o", 0, 3), ("T", 3, 1), ("Q", "o", 0, 1), ("T", 3, 2),
+    ("Q", "o", 0, 2), ("T", 3, 3), ("RGV", "o", 1, 0), ("MX1", 3, 1), ("SIL", 2, 3), ("GW", 3, 0),
+    ("Q", "o", 0, 3), ("MX1", 3, 2), ("ld", "o", 1, 2), ("GW", 3, 1), ("MUL", 2), ("GW", 3, 2), ("MX1", 3, 3),
+    ("GW", 3, 3), ("SIL", 3, 1), ("QH", 2), ("MX2", 0, 0), ("SIL", 3, 2), ("Q", "o", 1, 0), ("SIL", 3, 3),
+    ("RGV", "o", 1, 3), ("MX2", 0, 1), ("RGS", "o", 1, 1), ("MUL", 3), ("MX2", 0, 2), ("ld", "o", 1, 3),
+    ("RGS", "o", 1, 2), ("MX2", 1, 0), ("QH", 3), ("Q", "o", 1, 1), ("Q", "o", 1, 3), ("RGS", "o", 2, 0),
+    ("MX2", 0, 3), ("RGV", "o", 2, 2), ("MX2", 1, 1), ("Q", "o", 1, 2), ("J5", 0, 0), ("RGS", "o", 2, 1),
+    ("J5", 0, 1), ("MX2", 1, 2), ("st", 0, 0), ("J5", 0, 2), ("J5", 0, 3), ("st", 0, 1), ("MX2", 1, 3),
+    ("RGS", "o", 3, 0), ("Q", "o", 2, 0), ("st", 0, 2), ("Q", "o", 2, 1), ("st", 0, 3), ("Q", "o", 2, 2),
+    ("MX2", 2, 0), ("RGV", "o", 2, 3), ("RGS", "o", 3, 1), ("MX2", 2, 1), ("Q", "o", 2, 3), ("J5", 1, 0),
+    ("MX2", 2, 2), ("J5", 1, 1), ("RGS", "o", 3, 3), ("st", 1, 0), ("J5", 1, 2), ("J5", 1, 3), ("st", 1, 1),
+    ("MX2", 2, 3), ("Q", "o", 3, 0), ("st", 1, 2), ("Q", "o", 3, 1), ("st", 1, 3), ("RGV", "o", 3, 2),
+    ("MX2", 3, 0), ("Q", "o", 3, 2), ("MX2", 3, 1), ("Q", "o", 3, 3), ("J5", 2, 0), ("MX2", 3, 2),
+    ("J5", 2, 1), ("st", 2, 0), ("J5", 2, 2), ("J5", 2, 3), ("st", 2, 1), ("MX2", 3, 3), ("st", 2, 2),
+    ("st", 2, 3), ("J5", 3, 0), ("J5", 3, 1), ("st", 3, 0), ("J5", 3, 2), ("st", 3, 1), ("J5", 3, 3),
+    ("st", 3, 2), ("st", 3, 3),
 ]
 
 
@@ -74,7 +75,7 @@ def tile_multiscaleretention_pb_kernel(tc, x, attn, Wg, bg, gn_w, gn_b, Wo, bo, 
         codep = ctx.enter_context(tc.tile_pool(name="codep", bufs=6))
         normp = ctx.enter_context(tc.tile_pool(name="normp", bufs=6))
         gatep = ctx.enter_context(tc.tile_pool(name="gatep", bufs=2))
-        outp = ctx.enter_context(tc.tile_pool(name="outp", bufs=3))
+        outp = ctx.enter_context(tc.tile_pool(name="outp", bufs=6))
         psum = ctx.enter_context(tc.psum_pool(name="psum", bufs=8))
 
 

@@ -21,44 +21,43 @@ FLOPS = 2 * 2 * S * E * E
 ORDER = [
     ("ldA", 0), ("ld", "g", 0, 0), ("ldA", 1), ("bn", 0), ("ld", "g", 0, 1), ("RGS", "g", 0, 0),
     ("RGV", "g", 1, 0), ("ldA", 2), ("Q", "g", 1, 0), ("bn", 1), ("ld", "g", 0, 2), ("RGS", "g", 0, 1),
-    ("Q", "g", 0, 0), ("ldA", 3), ("bn", 2), ("ld", "g", 0, 3), ("RGS", "g", 1, 1), ("Q", "g", 0, 1),
-    ("RGV", "g", 0, 2), ("RGS", "g", 1, 2), ("ld", "x", 0, 0), ("bn", 3), ("ld", "x", 1, 0), ("sm",),
-    ("RGS", "g", 0, 3), ("Q", "g", 0, 2), ("Q", "g", 1, 1), ("Q", "g", 1, 2), ("ld", "g", 1, 0), ("sqrt",),
-    ("RGV", "g", 1, 3), ("xT", 0, 0), ("xT", 1, 0), ("recip",), ("Q", "g", 0, 3), ("XE", 0, 0), ("xT", 2, 0),
-    ("J4", 0, 0), ("XE", 1, 0), ("xT", 3, 0), ("J4", 0, 1), ("ld", "g", 1, 1), ("XE", 2, 0), ("J4", 0, 2),
-    ("xT", 0, 1), ("J4", 0, 3), ("XE", 3, 0), ("xT", 1, 1), ("Q", "g", 1, 3), ("XE", 0, 1), ("xT", 2, 1),
-    ("J4", 1, 0), ("XE", 1, 1), ("xT", 3, 1), ("J4", 1, 1), ("ld", "g", 1, 2), ("Qx", 0), ("XE", 2, 1),
-    ("T", 0, 0), ("Qx", 1), ("XE", 3, 1), ("T", 0, 1), ("Qx", 2), ("GW", 0, 0), ("T", 0, 2), ("Qx", 3),
-    ("GW", 0, 1), ("T", 0, 3), ("RGV", "g", 2, 0), ("ld", "g", 1, 3), ("GW", 0, 2), ("GW", 0, 3),
-    ("MX1", 0, 0), ("J4", 1, 2), ("RGS", "g", 2, 1), ("J4", 1, 3), ("Q", "g", 2, 0), ("MX1", 0, 1),
-    ("J4", 2, 0), ("ldbo",), ("RGV", "g", 2, 2), ("MX1", 0, 2), ("SIL", 0, 0), ("ld", "o", 0, 0),
-    ("Q", "g", 2, 1), ("SIL", 0, 1), ("MX1", 0, 3), ("Q", "g", 2, 2), ("RGS", "g", 3, 1), ("J4", 2, 1),
-    ("RGV", "g", 3, 0), ("T", 1, 0), ("ld", "o", 0, 1), ("T", 1, 1), ("Q", "g", 3, 0), ("SIL", 0, 2),
-    ("T", 1, 2), ("RGV", "g", 3, 2), ("SIL", 0, 3), ("T", 1, 3), ("GW", 1, 0), ("MX1", 1, 0),
-    ("Q", "g", 3, 1), ("ld", "o", 0, 2), ("GW", 1, 1), ("MUL", 0), ("GW", 1, 2), ("MX1", 1, 1), ("GW", 1, 3),
-    ("SIL", 1, 0), ("MX1", 1, 2), ("SIL", 1, 1), ("ld", "o", 0, 3), ("QH", 0), ("RGS", "g", 2, 3),
-    ("MX1", 1, 3), ("J4", 2, 2), ("J4", 2, 3), ("Q", "g", 3, 2), ("T", 2, 0), ("RGV", "g", 3, 3),
-    ("ld", "o", 1, 0), ("T", 2, 1), ("SIL", 1, 2), ("Q", "g", 3, 3), ("T", 2, 2), ("SIL", 1, 3),
-    ("Q", "g", 2, 3), ("T", 2, 3), ("GW", 2, 0), ("J4", 3, 0), ("GW", 2, 1), ("MX1", 3, 0), ("MUL", 1),
-    ("ld", "o", 1, 1), ("GW", 2, 2), ("GW", 2, 3), ("MX1", 2, 0), ("SIL", 3, 0), ("QH", 1),
-    ("RGS", "o", 0, 2), ("MX1", 2, 1), ("J4", 3, 1), ("J4", 3, 2), ("MX1", 2, 2), ("J4", 3, 3),
-    ("RGV", "o", 0, 0), ("SIL", 2, 0), ("MX1", 2, 3), ("SIL", 2, 1), ("Q", "o", 0, 0), ("SIL", 2, 2),
-    ("RGV", "o", 0, 1), ("T", 3, 0), ("RGS", "o", 0, 3), ("T", 3, 1), ("Q", "o", 0, 1), ("T", 3, 2),
-    ("Q", "o", 0, 2), ("T", 3, 3), ("RGV", "o", 1, 0), ("MX1", 3, 1), ("SIL", 2, 3), ("GW", 3, 0),
-    ("Q", "o", 0, 3), ("MX1", 3, 2), ("ld", "o", 1, 2), ("GW", 3, 1), ("MUL", 2), ("GW", 3, 2), ("MX1", 3, 3),
-    ("GW", 3, 3), ("SIL", 3, 1), ("QH", 2), ("MX2", 0, 0), ("SIL", 3, 2), ("Q", "o", 1, 0), ("SIL", 3, 3),
-    ("RGV", "o", 1, 3), ("MX2", 0, 1), ("RGS", "o", 1, 1), ("MUL", 3), ("MX2", 0, 2), ("ld", "o", 1, 3),
-    ("RGS", "o", 1, 2), ("MX2", 1, 0), ("QH", 3), ("Q", "o", 1, 1), ("Q", "o", 1, 3), ("RGS", "o", 2, 0),
-    ("MX2", 0, 3), ("RGV", "o", 2, 2), ("MX2", 1, 1), ("Q", "o", 1, 2), ("J5", 0, 0), ("RGS", "o", 2, 1),
-    ("J5", 0, 1), ("MX2", 1, 2), ("st", 0, 0), ("J5", 0, 2), ("J5", 0, 3), ("st", 0, 1), ("MX2", 1, 3),
-    ("RGS", "o", 3, 0), ("Q", "o", 2, 0), ("st", 0, 2), ("Q", "o", 2, 1), ("st", 0, 3), ("Q", "o", 2, 2),
-    ("MX2", 2, 0), ("RGV", "o", 2, 3), ("RGS", "o", 3, 1), ("MX2", 2, 1), ("Q", "o", 2, 3), ("J5", 1, 0),
-    ("MX2", 2, 2), ("J5", 1, 1), ("RGS", "o", 3, 3), ("st", 1, 0), ("J5", 1, 2), ("J5", 1, 3), ("st", 1, 1),
-    ("MX2", 2, 3), ("Q", "o", 3, 0), ("st", 1, 2), ("Q", "o", 3, 1), ("st", 1, 3), ("RGV", "o", 3, 2),
-    ("MX2", 3, 0), ("Q", "o", 3, 2), ("MX2", 3, 1), ("Q", "o", 3, 3), ("J5", 2, 0), ("MX2", 3, 2),
-    ("J5", 2, 1), ("st", 2, 0), ("J5", 2, 2), ("J5", 2, 3), ("st", 2, 1), ("MX2", 3, 3), ("st", 2, 2),
-    ("st", 2, 3), ("J5", 3, 0), ("J5", 3, 1), ("st", 3, 0), ("J5", 3, 2), ("st", 3, 1), ("J5", 3, 3),
-    ("st", 3, 2), ("st", 3, 3),
+    ("Q", "g", 0, 0), ("ldA", 3), ("RGV", "g", 1, 1), ("ld", "g", 0, 3), ("bn", 2), ("RGS", "g", 0, 2),
+    ("Q", "g", 0, 1), ("ld", "x", 0, 0), ("bn", 3), ("RGS", "g", 1, 2), ("ld", "x", 1, 0), ("sm",),
+    ("Q", "g", 0, 2), ("RGS", "g", 0, 3), ("Q", "g", 1, 1), ("Q", "g", 1, 2), ("ld", "g", 1, 0),
+    ("RGV", "g", 1, 3), ("xT", 0, 0), ("sqrt",), ("xT", 1, 0), ("recip",), ("XE", 0, 0), ("xT", 2, 0),
+    ("Q", "g", 0, 3), ("XE", 1, 0), ("xT", 3, 0), ("J4", 0, 0), ("ld", "g", 1, 1), ("XE", 2, 0), ("J4", 0, 1),
+    ("xT", 0, 1), ("J4", 0, 2), ("XE", 3, 0), ("xT", 1, 1), ("J4", 0, 3), ("XE", 0, 1), ("Q", "g", 1, 3),
+    ("xT", 2, 1), ("XE", 1, 1), ("xT", 3, 1), ("J4", 1, 0), ("ld", "g", 1, 2), ("Qx", 0), ("XE", 2, 1),
+    ("T", 0, 0), ("Qx", 1), ("XE", 3, 1), ("T", 0, 1), ("GW", 0, 0), ("Qx", 2), ("T", 0, 2), ("GW", 0, 1),
+    ("Qx", 3), ("T", 0, 3), ("ld", "g", 1, 3), ("GW", 0, 2), ("J4", 1, 1), ("RGV", "g", 2, 0), ("GW", 0, 3),
+    ("MX1", 0, 0), ("RGS", "g", 2, 1), ("J4", 1, 2), ("J4", 1, 3), ("MX1", 0, 1), ("ldbo",), ("Q", "g", 2, 0),
+    ("J4", 2, 0), ("MX1", 0, 2), ("SIL", 0, 0), ("J4", 2, 1), ("ld", "o", 0, 0), ("SIL", 0, 1),
+    ("Q", "g", 2, 1), ("MX1", 0, 3), ("RGS", "g", 2, 2), ("RGV", "g", 3, 0), ("RGV", "g", 2, 3), ("T", 1, 0),
+    ("ld", "o", 0, 1), ("T", 1, 1), ("SIL", 0, 2), ("Q", "g", 2, 3), ("T", 1, 2), ("SIL", 0, 3),
+    ("Q", "g", 2, 2), ("T", 1, 3), ("GW", 1, 0), ("MX1", 1, 0), ("Q", "g", 3, 0), ("ld", "o", 0, 2),
+    ("GW", 1, 1), ("MUL", 0), ("GW", 1, 2), ("MX1", 1, 1), ("GW", 1, 3), ("SIL", 1, 0), ("MX1", 1, 2),
+    ("QH", 0), ("RGS", "g", 3, 3), ("J4", 2, 2), ("MX1", 1, 3), ("J4", 2, 3), ("RGV", "g", 3, 1),
+    ("MX1", 2, 0), ("SIL", 1, 1), ("Q", "g", 3, 1), ("ld", "o", 0, 3), ("SIL", 1, 2), ("T", 2, 0),
+    ("RGV", "g", 3, 2), ("SIL", 1, 3), ("T", 2, 1), ("SIL", 2, 0), ("T", 2, 2), ("Q", "g", 3, 2),
+    ("GW", 2, 0), ("T", 2, 3), ("MUL", 1), ("ld", "o", 1, 0), ("GW", 2, 1), ("MX1", 2, 1), ("GW", 2, 2),
+    ("GW", 2, 3), ("MX1", 2, 2), ("RGS", "o", 0, 0), ("QH", 1), ("ld", "o", 1, 1), ("Q", "g", 3, 3),
+    ("MX1", 2, 3), ("J4", 3, 0), ("J4", 3, 1), ("SIL", 2, 1), ("MX1", 3, 0), ("J4", 3, 2), ("SIL", 2, 2),
+    ("J4", 3, 3), ("Q", "o", 0, 0), ("SIL", 2, 3), ("MX1", 3, 1), ("RGV", "o", 0, 1), ("RGS", "o", 0, 2),
+    ("T", 3, 0), ("MUL", 2), ("T", 3, 1), ("T", 3, 2), ("GW", 3, 0), ("T", 3, 3), ("GW", 3, 1), ("MX1", 3, 2),
+    ("QH", 2), ("GW", 3, 2), ("Q", "o", 0, 1), ("GW", 3, 3), ("MX1", 3, 3), ("Q", "o", 0, 2), ("SIL", 3, 0),
+    ("RGV", "o", 1, 0), ("SIL", 3, 1), ("MX2", 0, 0), ("SIL", 3, 2), ("Q", "o", 1, 0), ("SIL", 3, 3),
+    ("ld", "o", 1, 2), ("MX2", 0, 1), ("RGV", "o", 1, 1), ("RGS", "o", 0, 3), ("MUL", 3), ("MX2", 0, 2),
+    ("RGS", "o", 1, 2), ("MX2", 1, 0), ("ld", "o", 1, 3), ("QH", 3), ("Q", "o", 0, 3), ("RGS", "o", 1, 3),
+    ("Q", "o", 1, 1), ("Q", "o", 1, 2), ("MX2", 0, 3), ("RGV", "o", 2, 0), ("RGS", "o", 2, 2), ("MX2", 1, 1),
+    ("Q", "o", 2, 0), ("Q", "o", 1, 3), ("MX2", 1, 2), ("J5", 0, 0), ("J5", 0, 1), ("RGS", "o", 2, 3),
+    ("MX2", 1, 3), ("st", 0, 0), ("J5", 0, 2), ("st", 0, 1), ("J5", 0, 3), ("RGV", "o", 2, 1), ("st", 0, 2),
+    ("RGS", "o", 3, 0), ("MX2", 2, 0), ("st", 0, 3), ("Q", "o", 2, 1), ("Q", "o", 2, 2), ("Q", "o", 2, 3),
+    ("RGS", "o", 3, 1), ("MX2", 2, 1), ("J5", 1, 0), ("J5", 1, 1), ("MX2", 2, 2), ("st", 1, 0), ("J5", 1, 2),
+    ("st", 1, 1), ("J5", 1, 3), ("RGS", "o", 3, 3), ("MX2", 2, 3), ("Q", "o", 3, 0), ("st", 1, 2),
+    ("Q", "o", 3, 1), ("st", 1, 3), ("RGV", "o", 3, 2), ("MX2", 3, 0), ("Q", "o", 3, 2), ("MX2", 3, 1),
+    ("Q", "o", 3, 3), ("J5", 2, 0), ("MX2", 3, 2), ("J5", 2, 1), ("st", 2, 0), ("J5", 2, 2), ("MX2", 3, 3),
+    ("st", 2, 1), ("J5", 2, 3), ("st", 2, 2), ("st", 2, 3), ("J5", 3, 0), ("J5", 3, 1), ("st", 3, 0),
+    ("J5", 3, 2), ("st", 3, 1), ("J5", 3, 3), ("st", 3, 2), ("st", 3, 3),
 ]
 
 

@@ -21,43 +21,44 @@ FLOPS = 2 * 2 * S * E * E
 ORDER = [
     ("ldA", 0), ("ld", "g", 0, 0), ("ldA", 1), ("bn", 0), ("ld", "g", 0, 1), ("RGS", "g", 0, 0),
     ("RGV", "g", 1, 0), ("ldA", 2), ("Q", "g", 1, 0), ("bn", 1), ("ld", "g", 0, 2), ("RGS", "g", 0, 1),
-    ("Q", "g", 0, 0), ("ldA", 3), ("RGV", "g", 1, 1), ("ld", "g", 0, 3), ("bn", 2), ("RGS", "g", 0, 2),
-    ("Q", "g", 0, 1), ("ld", "x", 0, 0), ("bn", 3), ("RGS", "g", 1, 2), ("ld", "x", 1, 0), ("sm",),
-    ("Q", "g", 0, 2), ("RGS", "g", 0, 3), ("Q", "g", 1, 1), ("Q", "g", 1, 2), ("ld", "g", 1, 0),
-    ("RGV", "g", 1, 3), ("xT", 0, 0), ("sqrt",), ("xT", 1, 0), ("recip",), ("XE", 0, 0), ("xT", 2, 0),
-    ("Q", "g", 0, 3), ("XE", 1, 0), ("xT", 3, 0), ("J4", 0, 0), ("ld", "g", 1, 1), ("XE", 2, 0), ("J4", 0, 1),
-    ("xT", 0, 1), ("J4", 0, 2), ("XE", 3, 0), ("xT", 1, 1), ("J4", 0, 3), ("XE", 0, 1), ("Q", "g", 1, 3),
-    ("xT", 2, 1), ("XE", 1, 1), ("xT", 3, 1), ("J4", 1, 0), ("ld", "g", 1, 2), ("Qx", 0), ("XE", 2, 1),
-    ("T", 0, 0), ("Qx", 1), ("XE", 3, 1), ("T", 0, 1), ("GW", 0, 0), ("Qx", 2), ("T", 0, 2), ("GW", 0, 1),
-    ("Qx", 3), ("T", 0, 3), ("ld", "g", 1, 3), ("GW", 0, 2), ("J4", 1, 1), ("RGV", "g", 2, 0), ("GW", 0, 3),
-    ("MX1", 0, 0), ("RGS", "g", 2, 1), ("J4", 1, 2), ("J4", 1, 3), ("MX1", 0, 1), ("ldbo",), ("Q", "g", 2, 0),
-    ("J4", 2, 0), ("MX1", 0, 2), ("SIL", 0, 0), ("J4", 2, 1), ("ld", "o", 0, 0), ("SIL", 0, 1),
-    ("Q", "g", 2, 1), ("MX1", 0, 3), ("RGS", "g", 2, 2), ("RGV", "g", 3, 0), ("RGV", "g", 2, 3), ("T", 1, 0),
-    ("ld", "o", 0, 1), ("T", 1, 1), ("SIL", 0, 2), ("Q", "g", 2, 3), ("T", 1, 2), ("SIL", 0, 3),
-    ("Q", "g", 2, 2), ("T", 1, 3), ("GW", 1, 0), ("MX1", 1, 0), ("Q", "g", 3, 0), ("ld", "o", 0, 2),
-    ("GW", 1, 1), ("MUL", 0), ("GW", 1, 2), ("MX1", 1, 1), ("GW", 1, 3), ("SIL", 1, 0), ("MX1", 1, 2),
-    ("QH", 0), ("RGS", "g", 3, 3), ("J4", 2, 2), ("MX1", 1, 3), ("J4", 2, 3), ("RGV", "g", 3, 1),
-    ("MX1", 2, 0), ("SIL", 1, 1), ("Q", "g", 3, 1), ("ld", "o", 0, 3), ("SIL", 1, 2), ("T", 2, 0),
-    ("RGV", "g", 3, 2), ("SIL", 1, 3), ("T", 2, 1), ("SIL", 2, 0), ("T", 2, 2), ("Q", "g", 3, 2),
-    ("GW", 2, 0), ("T", 2, 3), ("MUL", 1), ("ld", "o", 1, 0), ("GW", 2, 1), ("MX1", 2, 1), ("GW", 2, 2),
-    ("GW", 2, 3), ("MX1", 2, 2), ("RGS", "o", 0, 0), ("QH", 1), ("ld", "o", 1, 1), ("Q", "g", 3, 3),
-    ("MX1", 2, 3), ("J4", 3, 0), ("J4", 3, 1), ("SIL", 2, 1), ("MX1", 3, 0), ("J4", 3, 2), ("SIL", 2, 2),
-    ("J4", 3, 3), ("Q", "o", 0, 0), ("SIL", 2, 3), ("MX1", 3, 1), ("RGV", "o", 0, 1), ("RGS", "o", 0, 2),
-    ("T", 3, 0), ("MUL", 2), ("T", 3, 1), ("T", 3, 2), ("GW", 3, 0), ("T", 3, 3), ("GW", 3, 1), ("MX1", 3, 2),
-    ("QH", 2), ("GW", 3, 2), ("Q", "o", 0, 1), ("GW", 3, 3), ("MX1", 3, 3), ("Q", "o", 0, 2), ("SIL", 3, 0),
-    ("RGV", "o", 1, 0), ("SIL", 3, 1), ("MX2", 0, 0), ("SIL", 3, 2), ("Q", "o", 1, 0), ("SIL", 3, 3),
-    ("ld", "o", 1, 2), ("MX2", 0, 1), ("RGV", "o", 1, 1), ("RGS", "o", 0, 3), ("MUL", 3), ("MX2", 0, 2),
-    ("RGS", "o", 1, 2), ("MX2", 1, 0), ("ld", "o", 1, 3), ("QH", 3), ("Q", "o", 0, 3), ("RGS", "o", 1, 3),
-    ("Q", "o", 1, 1), ("Q", "o", 1, 2), ("MX2", 0, 3), ("RGV", "o", 2, 0), ("RGS", "o", 2, 2), ("MX2", 1, 1),
-    ("Q", "o", 2, 0), ("Q", "o", 1, 3), ("MX2", 1, 2), ("J5", 0, 0), ("J5", 0, 1), ("RGS", "o", 2, 3),
-    ("MX2", 1, 3), ("st", 0, 0), ("J5", 0, 2), ("st", 0, 1), ("J5", 0, 3), ("RGV", "o", 2, 1), ("st", 0, 2),
-    ("RGS", "o", 3, 0), ("MX2", 2, 0), ("st", 0, 3), ("Q", "o", 2, 1), ("Q", "o", 2, 2), ("Q", "o", 2, 3),
-    ("RGS", "o", 3, 1), ("MX2", 2, 1), ("J5", 1, 0), ("J5", 1, 1), ("MX2", 2, 2), ("st", 1, 0), ("J5", 1, 2),
-    ("st", 1, 1), ("J5", 1, 3), ("RGS", "o", 3, 3), ("MX2", 2, 3), ("Q", "o", 3, 0), ("st", 1, 2),
-    ("Q", "o", 3, 1), ("st", 1, 3), ("RGV", "o", 3, 2), ("MX2", 3, 0), ("Q", "o", 3, 2), ("MX2", 3, 1),
-    ("Q", "o", 3, 3), ("J5", 2, 0), ("MX2", 3, 2), ("J5", 2, 1), ("st", 2, 0), ("J5", 2, 2), ("MX2", 3, 3),
-    ("st", 2, 1), ("J5", 2, 3), ("st", 2, 2), ("st", 2, 3), ("J5", 3, 0), ("J5", 3, 1), ("st", 3, 0),
-    ("J5", 3, 2), ("st", 3, 1), ("J5", 3, 3), ("st", 3, 2), ("st", 3, 3),
+    ("Q", "g", 0, 0), ("ldA", 3), ("bn", 2), ("ld", "g", 0, 3), ("RGS", "g", 1, 1), ("Q", "g", 0, 1),
+    ("RGV", "g", 1, 2), ("ld", "x", 0, 0), ("RGS", "g", 0, 2), ("bn", 3), ("ld", "x", 1, 0), ("sm",),
+    ("RGS", "g", 0, 3), ("Q", "g", 0, 2), ("Q", "g", 1, 1), ("Q", "g", 1, 2), ("ld", "g", 1, 0),
+    ("RGV", "g", 1, 3), ("sqrt",), ("xT", 0, 0), ("xT", 1, 0), ("recip",), ("Q", "g", 0, 3), ("XE", 0, 0),
+    ("xT", 2, 0), ("J4", 0, 0), ("XE", 1, 0), ("xT", 3, 0), ("J4", 0, 1), ("ld", "g", 1, 1), ("XE", 2, 0),
+    ("J4", 0, 2), ("xT", 0, 1), ("J4", 0, 3), ("XE", 3, 0), ("xT", 1, 1), ("Q", "g", 1, 3), ("XE", 0, 1),
+    ("xT", 2, 1), ("J4", 1, 0), ("xT", 3, 1), ("J4", 1, 1), ("XE", 1, 1), ("ld", "g", 1, 2), ("Qx", 0),
+    ("T", 0, 0), ("XE", 2, 1), ("RGV", "g", 3, 0), ("T", 0, 1), ("XE", 3, 1), ("T", 0, 2), ("GW", 0, 0),
+    ("Qx", 1), ("T", 0, 3), ("GW", 0, 1), ("Qx", 2), ("ld", "g", 1, 3), ("GW", 0, 2), ("Qx", 3), ("J4", 1, 2),
+    ("GW", 0, 3), ("J4", 1, 3), ("RGS", "g", 2, 0), ("J4", 2, 0), ("MX1", 0, 0), ("J4", 2, 1), ("ldbo",),
+    ("RGV", "g", 2, 2), ("MX1", 0, 1), ("ld", "o", 0, 0), ("Q", "g", 2, 2), ("SIL", 0, 0), ("MX1", 0, 2),
+    ("Q", "g", 3, 0), ("RGS", "g", 2, 1), ("Q", "g", 2, 0), ("MX1", 0, 3), ("RGV", "g", 2, 3),
+    ("ld", "o", 0, 1), ("Q", "g", 2, 3), ("T", 1, 0), ("SIL", 0, 1), ("RGV", "g", 3, 1), ("T", 1, 1),
+    ("SIL", 0, 2), ("T", 1, 2), ("Q", "g", 2, 1), ("ld", "o", 0, 2), ("T", 1, 3), ("SIL", 0, 3),
+    ("Q", "g", 3, 1), ("MX1", 1, 0), ("GW", 1, 0), ("RGV", "g", 3, 2), ("GW", 1, 1), ("MX1", 1, 1),
+    ("MUL", 0), ("GW", 1, 2), ("ld", "o", 0, 3), ("GW", 1, 3), ("MX1", 1, 2), ("SIL", 1, 0), ("QH", 0),
+    ("MX1", 1, 3), ("SIL", 1, 1), ("J4", 2, 2), ("ld", "o", 1, 0), ("SIL", 1, 2), ("J4", 2, 3), ("MX1", 2, 0),
+    ("Q", "g", 3, 2), ("RGS", "o", 0, 0), ("RGV", "g", 3, 3), ("T", 2, 0), ("T", 2, 1), ("Q", "g", 3, 3),
+    ("T", 2, 2), ("ld", "o", 1, 1), ("J4", 3, 0), ("SIL", 1, 3), ("J4", 3, 1), ("T", 2, 3), ("GW", 2, 0),
+    ("Q", "o", 0, 0), ("MX1", 2, 1), ("MUL", 1), ("GW", 2, 1), ("GW", 2, 2), ("MX1", 2, 2), ("GW", 2, 3),
+    ("MX1", 2, 3), ("QH", 1), ("SIL", 2, 0), ("J4", 3, 2), ("SIL", 2, 1), ("J4", 3, 3), ("MX1", 3, 0),
+    ("SIL", 2, 2), ("RGV", "o", 0, 1), ("SIL", 2, 3), ("T", 3, 0), ("Q", "o", 0, 1), ("SIL", 3, 0),
+    ("T", 3, 1), ("RGV", "o", 0, 2), ("T", 3, 2), ("GW", 3, 0), ("T", 3, 3), ("MUL", 2), ("GW", 3, 1),
+    ("MX1", 3, 1), ("GW", 3, 2), ("GW", 3, 3), ("MX1", 3, 2), ("QH", 2), ("SIL", 3, 1), ("Q", "o", 0, 2),
+    ("MX1", 3, 3), ("RGS", "o", 1, 1), ("RGV", "o", 0, 3), ("MX2", 0, 0), ("Q", "o", 0, 3),
+    ("RGV", "o", 1, 0), ("SIL", 3, 2), ("MX2", 0, 1), ("ld", "o", 1, 2), ("SIL", 3, 3), ("Q", "o", 1, 0),
+    ("MX2", 0, 2), ("RGS", "o", 2, 0), ("Q", "o", 1, 1), ("MUL", 3), ("MX2", 1, 0), ("ld", "o", 1, 3),
+    ("RGS", "o", 2, 1), ("MX2", 1, 1), ("QH", 3), ("RGV", "o", 1, 2), ("MX2", 0, 3), ("Q", "o", 1, 2),
+    ("RGS", "o", 2, 2), ("RGV", "o", 1, 3), ("MX2", 1, 2), ("Q", "o", 1, 3), ("J5", 0, 0), ("RGS", "o", 2, 3),
+    ("J5", 0, 1), ("MX2", 1, 3), ("st", 0, 0), ("J5", 0, 2), ("J5", 0, 3), ("st", 0, 1), ("Q", "o", 2, 0),
+    ("st", 0, 2), ("RGS", "o", 3, 0), ("Q", "o", 2, 1), ("st", 0, 3), ("Q", "o", 2, 2), ("MX2", 2, 0),
+    ("Q", "o", 2, 3), ("J5", 1, 0), ("RGS", "o", 3, 1), ("MX2", 2, 1), ("J5", 1, 1), ("st", 1, 0),
+    ("J5", 1, 2), ("MX2", 2, 2), ("J5", 1, 3), ("st", 1, 1), ("Q", "o", 3, 0), ("st", 1, 2),
+    ("RGS", "o", 3, 3), ("RGV", "o", 3, 2), ("MX2", 2, 3), ("st", 1, 3), ("Q", "o", 3, 1), ("MX2", 3, 0),
+    ("Q", "o", 3, 2), ("J5", 2, 0), ("MX2", 3, 1), ("Q", "o", 3, 3), ("st", 2, 0), ("J5", 2, 1),
+    ("MX2", 3, 2), ("J5", 2, 2), ("st", 2, 1), ("J5", 2, 3), ("MX2", 3, 3), ("st", 2, 2), ("st", 2, 3),
+    ("J5", 3, 0), ("J5", 3, 1), ("st", 3, 0), ("J5", 3, 2), ("J5", 3, 3), ("st", 3, 1), ("st", 3, 2),
+    ("st", 3, 3),
 ]
 
 

@@ -22,43 +22,43 @@ ORDER = [
     ("ldA", 0), ("ld", "g", 0, 0), ("ldA", 1), ("bn", 0), ("ld", "g", 0, 1), ("RGS", "g", 0, 0),
     ("RGV", "g", 1, 0), ("ldA", 2), ("Q", "g", 1, 0), ("bn", 1), ("ld", "g", 0, 2), ("RGS", "g", 0, 1),
     ("Q", "g", 0, 0), ("ldA", 3), ("bn", 2), ("ld", "g", 0, 3), ("RGS", "g", 1, 1), ("Q", "g", 0, 1),
-    ("RGV", "g", 1, 2), ("ld", "x", 0, 0), ("RGS", "g", 0, 2), ("bn", 3), ("ld", "x", 1, 0), ("sm",),
-    ("RGS", "g", 0, 3), ("Q", "g", 0, 2), ("Q", "g", 1, 1), ("Q", "g", 1, 2), ("ld", "g", 1, 0),
-    ("RGV", "g", 1, 3), ("sqrt",), ("xT", 0, 0), ("xT", 1, 0), ("recip",), ("Q", "g", 0, 3), ("XE", 0, 0),
-    ("xT", 2, 0), ("J4", 0, 0), ("XE", 1, 0), ("xT", 3, 0), ("J4", 0, 1), ("ld", "g", 1, 1), ("XE", 2, 0),
-    ("J4", 0, 2), ("xT", 0, 1), ("J4", 0, 3), ("XE", 3, 0), ("xT", 1, 1), ("Q", "g", 1, 3), ("XE", 0, 1),
-    ("xT", 2, 1), ("J4", 1, 0), ("xT", 3, 1), ("J4", 1, 1), ("XE", 1, 1), ("ld", "g", 1, 2), ("Qx", 0),
-    ("T", 0, 0), ("XE", 2, 1), ("RGV", "g", 3, 0), ("T", 0, 1), ("XE", 3, 1), ("T", 0, 2), ("GW", 0, 0),
-    ("Qx", 1), ("T", 0, 3), ("GW", 0, 1), ("Qx", 2), ("ld", "g", 1, 3), ("GW", 0, 2), ("Qx", 3), ("J4", 1, 2),
-    ("GW", 0, 3), ("J4", 1, 3), ("RGS", "g", 2, 0), ("J4", 2, 0), ("MX1", 0, 0), ("J4", 2, 1), ("ldbo",),
-    ("RGV", "g", 2, 2), ("MX1", 0, 1), ("ld", "o", 0, 0), ("Q", "g", 2, 2), ("SIL", 0, 0), ("MX1", 0, 2),
-    ("Q", "g", 3, 0), ("RGS", "g", 2, 1), ("Q", "g", 2, 0), ("MX1", 0, 3), ("RGV", "g", 2, 3),
-    ("ld", "o", 0, 1), ("Q", "g", 2, 3), ("T", 1, 0), ("SIL", 0, 1), ("RGV", "g", 3, 1), ("T", 1, 1),
-    ("SIL", 0, 2), ("T", 1, 2), ("Q", "g", 2, 1), ("ld", "o", 0, 2), ("T", 1, 3), ("SIL", 0, 3),
-    ("Q", "g", 3, 1), ("MX1", 1, 0), ("GW", 1, 0), ("RGV", "g", 3, 2), ("GW", 1, 1), ("MX1", 1, 1),
-    ("MUL", 0), ("GW", 1, 2), ("ld", "o", 0, 3), ("GW", 1, 3), ("MX1", 1, 2), ("SIL", 1, 0), ("QH", 0),
-    ("MX1", 1, 3), ("SIL", 1, 1), ("J4", 2, 2), ("ld", "o", 1, 0), ("SIL", 1, 2), ("J4", 2, 3), ("MX1", 2, 0),
-    ("Q", "g", 3, 2), ("RGS", "o", 0, 0), ("RGV", "g", 3, 3), ("T", 2, 0), ("T", 2, 1), ("Q", "g", 3, 3),
-    ("T", 2, 2), ("ld", "o", 1, 1), ("J4", 3, 0), ("SIL", 1, 3), ("J4", 3, 1), ("T", 2, 3), ("GW", 2, 0),
-    ("Q", "o", 0, 0), ("MX1", 2, 1), ("MUL", 1), ("GW", 2, 1), ("GW", 2, 2), ("MX1", 2, 2), ("GW", 2, 3),
-    ("MX1", 2, 3), ("QH", 1), ("SIL", 2, 0), ("J4", 3, 2), ("SIL", 2, 1), ("J4", 3, 3), ("MX1", 3, 0),
-    ("SIL", 2, 2), ("RGV", "o", 0, 1), ("SIL", 2, 3), ("T", 3, 0), ("Q", "o", 0, 1), ("SIL", 3, 0),
-    ("T", 3, 1), ("RGV", "o", 0, 2), ("T", 3, 2), ("GW", 3, 0), ("T", 3, 3), ("MUL", 2), ("GW", 3, 1),
-    ("MX1", 3, 1), ("GW", 3, 2), ("GW", 3, 3), ("MX1", 3, 2), ("QH", 2), ("SIL", 3, 1), ("Q", "o", 0, 2),
-    ("MX1", 3, 3), ("RGS", "o", 1, 1), ("RGV", "o", 0, 3), ("MX2", 0, 0), ("Q", "o", 0, 3),
-    ("RGV", "o", 1, 0), ("SIL", 3, 2), ("MX2", 0, 1), ("ld", "o", 1, 2), ("SIL", 3, 3), ("Q", "o", 1, 0),
-    ("MX2", 0, 2), ("RGS", "o", 2, 0), ("Q", "o", 1, 1), ("MUL", 3), ("MX2", 1, 0), ("ld", "o", 1, 3),
-    ("RGS", "o", 2, 1), ("MX2", 1, 1), ("QH", 3), ("RGV", "o", 1, 2), ("MX2", 0, 3), ("Q", "o", 1, 2),
-    ("RGS", "o", 2, 2), ("RGV", "o", 1, 3), ("MX2", 1, 2), ("Q", "o", 1, 3), ("J5", 0, 0), ("RGS", "o", 2, 3),
-    ("J5", 0, 1), ("MX2", 1, 3), ("st", 0, 0), ("J5", 0, 2), ("J5", 0, 3), ("st", 0, 1), ("Q", "o", 2, 0),
-    ("st", 0, 2), ("RGS", "o", 3, 0), ("Q", "o", 2, 1), ("st", 0, 3), ("Q", "o", 2, 2), ("MX2", 2, 0),
-    ("Q", "o", 2, 3), ("J5", 1, 0), ("RGS", "o", 3, 1), ("MX2", 2, 1), ("J5", 1, 1), ("st", 1, 0),
-    ("J5", 1, 2), ("MX2", 2, 2), ("J5", 1, 3), ("st", 1, 1), ("Q", "o", 3, 0), ("st", 1, 2),
-    ("RGS", "o", 3, 3), ("RGV", "o", 3, 2), ("MX2", 2, 3), ("st", 1, 3), ("Q", "o", 3, 1), ("MX2", 3, 0),
-    ("Q", "o", 3, 2), ("J5", 2, 0), ("MX2", 3, 1), ("Q", "o", 3, 3), ("st", 2, 0), ("J5", 2, 1),
-    ("MX2", 3, 2), ("J5", 2, 2), ("st", 2, 1), ("J5", 2, 3), ("MX2", 3, 3), ("st", 2, 2), ("st", 2, 3),
-    ("J5", 3, 0), ("J5", 3, 1), ("st", 3, 0), ("J5", 3, 2), ("J5", 3, 3), ("st", 3, 1), ("st", 3, 2),
-    ("st", 3, 3),
+    ("RGV", "g", 0, 2), ("RGS", "g", 1, 2), ("ld", "x", 0, 0), ("bn", 3), ("ld", "x", 1, 0), ("sm",),
+    ("RGS", "g", 0, 3), ("Q", "g", 0, 2), ("Q", "g", 1, 1), ("Q", "g", 1, 2), ("ld", "g", 1, 0), ("sqrt",),
+    ("RGV", "g", 1, 3), ("xT", 0, 0), ("xT", 1, 0), ("recip",), ("Q", "g", 0, 3), ("XE", 0, 0), ("xT", 2, 0),
+    ("J4", 0, 0), ("XE", 1, 0), ("xT", 3, 0), ("J4", 0, 1), ("ld", "g", 1, 1), ("XE", 2, 0), ("J4", 0, 2),
+    ("xT", 0, 1), ("J4", 0, 3), ("XE", 3, 0), ("xT", 1, 1), ("Q", "g", 1, 3), ("XE", 0, 1), ("xT", 2, 1),
+    ("J4", 1, 0), ("XE", 1, 1), ("xT", 3, 1), ("J4", 1, 1), ("ld", "g", 1, 2), ("Qx", 0), ("XE", 2, 1),
+    ("T", 0, 0), ("Qx", 1), ("XE", 3, 1), ("T", 0, 1), ("Qx", 2), ("GW", 0, 0), ("T", 0, 2), ("Qx", 3),
+    ("GW", 0, 1), ("T", 0, 3), ("RGV", "g", 2, 0), ("ld", "g", 1, 3), ("GW", 0, 2), ("GW", 0, 3),
+    ("MX1", 0, 0), ("J4", 1, 2), ("RGS", "g", 2, 1), ("J4", 1, 3), ("Q", "g", 2, 0), ("MX1", 0, 1),
+    ("J4", 2, 0), ("ldbo",), ("RGV", "g", 2, 2), ("MX1", 0, 2), ("SIL", 0, 0), ("ld", "o", 0, 0),
+    ("Q", "g", 2, 1), ("SIL", 0, 1), ("MX1", 0, 3), ("Q", "g", 2, 2), ("RGS", "g", 3, 1), ("J4", 2, 1),
+    ("RGV", "g", 3, 0), ("T", 1, 0), ("ld", "o", 0, 1), ("T", 1, 1), ("Q", "g", 3, 0), ("SIL", 0, 2),
+    ("T", 1, 2), ("RGV", "g", 3, 2), ("SIL", 0, 3), ("T", 1, 3), ("GW", 1, 0), ("MX1", 1, 0),
+    ("Q", "g", 3, 1), ("ld", "o", 0, 2), ("GW", 1, 1), ("MUL", 0), ("GW", 1, 2), ("MX1", 1, 1), ("GW", 1, 3),
+    ("SIL", 1, 0), ("MX1", 1, 2), ("SIL", 1, 1), ("ld", "o", 0, 3), ("QH", 0), ("RGS", "g", 2, 3),
+    ("MX1", 1, 3), ("J4", 2, 2), ("J4", 2, 3), ("Q", "g", 3, 2), ("T", 2, 0), ("RGV", "g", 3, 3),
+    ("ld", "o", 1, 0), ("T", 2, 1), ("SIL", 1, 2), ("Q", "g", 3, 3), ("T", 2, 2), ("SIL", 1, 3),
+    ("Q", "g", 2, 3), ("T", 2, 3), ("GW", 2, 0), ("J4", 3, 0), ("GW", 2, 1), ("MX1", 3, 0), ("MUL", 1),
+    ("ld", "o", 1, 1), ("GW", 2, 2), ("GW", 2, 3), ("MX1", 2, 0), ("SIL", 3, 0), ("QH", 1),
+    ("RGS", "o", 0, 2), ("MX1", 2, 1), ("J4", 3, 1), ("J4", 3, 2), ("MX1", 2, 2), ("J4", 3, 3),
+    ("RGV", "o", 0, 0), ("SIL", 2, 0), ("MX1", 2, 3), ("SIL", 2, 1), ("Q", "o", 0, 0), ("SIL", 2, 2),
+    ("RGV", "o", 0, 1), ("T", 3, 0), ("RGS", "o", 0, 3), ("T", 3, 1), ("Q", "o", 0, 1), ("T", 3, 2),
+    ("Q", "o", 0, 2), ("T", 3, 3), ("RGV", "o", 1, 0), ("MX1", 3, 1), ("SIL", 2, 3), ("GW", 3, 0),
+    ("Q", "o", 0, 3), ("MX1", 3, 2), ("ld", "o", 1, 2), ("GW", 3, 1), ("MUL", 2), ("GW", 3, 2), ("MX1", 3, 3),
+    ("GW", 3, 3), ("SIL", 3, 1), ("QH", 2), ("MX2", 0, 0), ("SIL", 3, 2), ("Q", "o", 1, 0), ("SIL", 3, 3),
+    ("RGV", "o", 1, 3), ("MX2", 0, 1), ("RGS", "o", 1, 1), ("MUL", 3), ("MX2", 0, 2), ("ld", "o", 1, 3),
+    ("RGS", "o", 1, 2), ("MX2", 1, 0), ("QH", 3), ("Q", "o", 1, 1), ("Q", "o", 1, 3), ("RGS", "o", 2, 0),
+    ("MX2", 0, 3), ("RGV", "o", 2, 2), ("MX2", 1, 1), ("Q", "o", 1, 2), ("J5", 0, 0), ("RGS", "o", 2, 1),
+    ("J5", 0, 1), ("MX2", 1, 2), ("st", 0, 0), ("J5", 0, 2), ("J5", 0, 3), ("st", 0, 1), ("MX2", 1, 3),
+    ("RGS", "o", 3, 0), ("Q", "o", 2, 0), ("st", 0, 2), ("Q", "o", 2, 1), ("st", 0, 3), ("Q", "o", 2, 2),
+    ("MX2", 2, 0), ("RGV", "o", 2, 3), ("RGS", "o", 3, 1), ("MX2", 2, 1), ("Q", "o", 2, 3), ("J5", 1, 0),
+    ("MX2", 2, 2), ("J5", 1, 1), ("RGS", "o", 3, 3), ("st", 1, 0), ("J5", 1, 2), ("J5", 1, 3), ("st", 1, 1),
+    ("MX2", 2, 3), ("Q", "o", 3, 0), ("st", 1, 2), ("Q", "o", 3, 1), ("st", 1, 3), ("RGV", "o", 3, 2),
+    ("MX2", 3, 0), ("Q", "o", 3, 2), ("MX2", 3, 1), ("Q", "o", 3, 3), ("J5", 2, 0), ("MX2", 3, 2),
+    ("J5", 2, 1), ("st", 2, 0), ("J5", 2, 2), ("J5", 2, 3), ("st", 2, 1), ("MX2", 3, 3), ("st", 2, 2),
+    ("st", 2, 3), ("J5", 3, 0), ("J5", 3, 1), ("st", 3, 0), ("J5", 3, 2), ("st", 3, 1), ("J5", 3, 3),
+    ("st", 3, 2), ("st", 3, 3),
 ]
 
 
@@ -77,6 +77,7 @@ def tile_multiscaleretention_pb_kernel(tc, x, attn, Wg, bg, gn_w, gn_b, Wo, bo, 
         gatep = ctx.enter_context(tc.tile_pool(name="gatep", bufs=2))
         outp = ctx.enter_context(tc.tile_pool(name="outp", bufs=6))
         psum = ctx.enter_context(tc.psum_pool(name="psum", bufs=8))
+        ctx.enter_context(tc.manual_schedule())
 
 
         ident = const.tile([P, P], F32, name="ident")

@@ -15,51 +15,32 @@ P = 128
 S = 512
 E = 2048
 EPS = 1e-5
-NPASS = E // 512
+PACK = 4
+K_PASS = P * PACK
+K_HALF = K_PASS // 2
+PASSES = E // K_PASS
+PANEL = 512
+TILES = 4
+GROUPS = E // P
+LOAD_COLS = 2 * PANEL
+RUN = 4
 FLOPS = 2 * 2 * S * E * E
 
-ORDER = [
-    ("ldA", 0), ("ld", "g", 0, 0), ("ldA", 1), ("bn", 0), ("ld", "g", 0, 1), ("RGS", "g", 0, 0),
-    ("RGV", "g", 1, 0), ("ldA", 2), ("Q", "g", 1, 0), ("bn", 1), ("ld", "g", 0, 2), ("RGS", "g", 0, 1),
-    ("Q", "g", 0, 0), ("ldA", 3), ("bn", 2), ("ld", "g", 0, 3), ("RGS", "g", 1, 1), ("Q", "g", 0, 1),
-    ("RGV", "g", 0, 2), ("RGS", "g", 1, 2), ("ld", "x", 0, 0), ("bn", 3), ("ld", "x", 1, 0), ("sm",),
-    ("RGS", "g", 0, 3), ("Q", "g", 0, 2), ("Q", "g", 1, 1), ("Q", "g", 1, 2), ("ld", "g", 1, 0), ("sqrt",),
-    ("RGV", "g", 1, 3), ("xT", 0, 0), ("xT", 1, 0), ("recip",), ("Q", "g", 0, 3), ("XE", 0, 0), ("xT", 2, 0),
-    ("J4", 0, 0), ("XE", 1, 0), ("xT", 3, 0), ("J4", 0, 1), ("ld", "g", 1, 1), ("XE", 2, 0), ("J4", 0, 2),
-    ("xT", 0, 1), ("J4", 0, 3), ("XE", 3, 0), ("xT", 1, 1), ("Q", "g", 1, 3), ("XE", 0, 1), ("xT", 2, 1),
-    ("J4", 1, 0), ("XE", 1, 1), ("xT", 3, 1), ("J4", 1, 1), ("ld", "g", 1, 2), ("Qx", 0), ("XE", 2, 1),
-    ("T", 0, 0), ("Qx", 1), ("XE", 3, 1), ("T", 0, 1), ("Qx", 2), ("GW", 0, 0), ("T", 0, 2), ("Qx", 3),
-    ("GW", 0, 1), ("T", 0, 3), ("RGV", "g", 2, 0), ("ld", "g", 1, 3), ("GW", 0, 2), ("GW", 0, 3),
-    ("MX1", 0, 0), ("J4", 1, 2), ("RGS", "g", 2, 1), ("J4", 1, 3), ("Q", "g", 2, 0), ("MX1", 0, 1),
-    ("J4", 2, 0), ("ldbo",), ("RGV", "g", 2, 2), ("MX1", 0, 2), ("SIL", 0, 0), ("ld", "o", 0, 0),
-    ("Q", "g", 2, 1), ("SIL", 0, 1), ("MX1", 0, 3), ("Q", "g", 2, 2), ("RGS", "g", 3, 1), ("J4", 2, 1),
-    ("RGV", "g", 3, 0), ("T", 1, 0), ("ld", "o", 0, 1), ("T", 1, 1), ("Q", "g", 3, 0), ("SIL", 0, 2),
-    ("T", 1, 2), ("RGV", "g", 3, 2), ("SIL", 0, 3), ("T", 1, 3), ("GW", 1, 0), ("MX1", 1, 0),
-    ("Q", "g", 3, 1), ("ld", "o", 0, 2), ("GW", 1, 1), ("MUL", 0), ("GW", 1, 2), ("MX1", 1, 1), ("GW", 1, 3),
-    ("SIL", 1, 0), ("MX1", 1, 2), ("SIL", 1, 1), ("ld", "o", 0, 3), ("QH", 0), ("RGS", "g", 2, 3),
-    ("MX1", 1, 3), ("J4", 2, 2), ("J4", 2, 3), ("Q", "g", 3, 2), ("T", 2, 0), ("RGV", "g", 3, 3),
-    ("ld", "o", 1, 0), ("T", 2, 1), ("SIL", 1, 2), ("Q", "g", 3, 3), ("T", 2, 2), ("SIL", 1, 3),
-    ("Q", "g", 2, 3), ("T", 2, 3), ("GW", 2, 0), ("J4", 3, 0), ("GW", 2, 1), ("MX1", 3, 0), ("MUL", 1),
-    ("ld", "o", 1, 1), ("GW", 2, 2), ("GW", 2, 3), ("MX1", 2, 0), ("SIL", 3, 0), ("QH", 1),
-    ("RGS", "o", 0, 2), ("MX1", 2, 1), ("J4", 3, 1), ("J4", 3, 2), ("MX1", 2, 2), ("J4", 3, 3),
-    ("RGV", "o", 0, 0), ("SIL", 2, 0), ("MX1", 2, 3), ("SIL", 2, 1), ("Q", "o", 0, 0), ("SIL", 2, 2),
-    ("RGV", "o", 0, 1), ("T", 3, 0), ("RGS", "o", 0, 3), ("T", 3, 1), ("Q", "o", 0, 1), ("T", 3, 2),
-    ("Q", "o", 0, 2), ("T", 3, 3), ("RGV", "o", 1, 0), ("MX1", 3, 1), ("SIL", 2, 3), ("GW", 3, 0),
-    ("Q", "o", 0, 3), ("MX1", 3, 2), ("ld", "o", 1, 2), ("GW", 3, 1), ("MUL", 2), ("GW", 3, 2), ("MX1", 3, 3),
-    ("GW", 3, 3), ("SIL", 3, 1), ("QH", 2), ("MX2", 0, 0), ("SIL", 3, 2), ("Q", "o", 1, 0), ("SIL", 3, 3),
-    ("RGV", "o", 1, 3), ("MX2", 0, 1), ("RGS", "o", 1, 1), ("MUL", 3), ("MX2", 0, 2), ("ld", "o", 1, 3),
-    ("RGS", "o", 1, 2), ("MX2", 1, 0), ("QH", 3), ("Q", "o", 1, 1), ("Q", "o", 1, 3), ("RGS", "o", 2, 0),
-    ("MX2", 0, 3), ("RGV", "o", 2, 2), ("MX2", 1, 1), ("Q", "o", 1, 2), ("J5", 0, 0), ("RGS", "o", 2, 1),
-    ("J5", 0, 1), ("MX2", 1, 2), ("st", 0, 0), ("J5", 0, 2), ("J5", 0, 3), ("st", 0, 1), ("MX2", 1, 3),
-    ("RGS", "o", 3, 0), ("Q", "o", 2, 0), ("st", 0, 2), ("Q", "o", 2, 1), ("st", 0, 3), ("Q", "o", 2, 2),
-    ("MX2", 2, 0), ("RGV", "o", 2, 3), ("RGS", "o", 3, 1), ("MX2", 2, 1), ("Q", "o", 2, 3), ("J5", 1, 0),
-    ("MX2", 2, 2), ("J5", 1, 1), ("RGS", "o", 3, 3), ("st", 1, 0), ("J5", 1, 2), ("J5", 1, 3), ("st", 1, 1),
-    ("MX2", 2, 3), ("Q", "o", 3, 0), ("st", 1, 2), ("Q", "o", 3, 1), ("st", 1, 3), ("RGV", "o", 3, 2),
-    ("MX2", 3, 0), ("Q", "o", 3, 2), ("MX2", 3, 1), ("Q", "o", 3, 3), ("J5", 2, 0), ("MX2", 3, 2),
-    ("J5", 2, 1), ("st", 2, 0), ("J5", 2, 2), ("J5", 2, 3), ("st", 2, 1), ("MX2", 3, 3), ("st", 2, 2),
-    ("st", 2, 3), ("J5", 3, 0), ("J5", 3, 1), ("st", 3, 0), ("J5", 3, 2), ("st", 3, 1), ("J5", 3, 3),
-    ("st", 3, 2), ("st", 3, 3),
-]
+RAW_BUFS = 6
+GROUPED_BUFS = 5
+CODE_BUFS = 6
+NORM_BUFS = 8
+GATE_BUFS = 2
+OUT_BUFS = 6
+PSUM_BANKS = 8
+
+
+def on_vector(kind, panel, c):
+    if kind == "g" and panel < 2:
+        return c == PASSES - 1
+    if kind == "g" or panel < 2:
+        return c < PASSES - 1
+    return panel == 2 and c < 2
 
 
 def tile_multiscaleretention_pb_kernel(tc, x, attn, Wg, bg, gn_w, gn_b, Wo, bo, out):
@@ -70,15 +51,13 @@ def tile_multiscaleretention_pb_kernel(tc, x, attn, Wg, bg, gn_w, gn_b, Wo, bo, 
 
     with ExitStack() as ctx:
         const = ctx.enter_context(tc.tile_pool(name="const", bufs=1))
-        rawp = ctx.enter_context(tc.tile_pool(name="rawp", bufs=6))
-        grpp = ctx.enter_context(tc.tile_pool(name="grpp", bufs=5))
-        codep = ctx.enter_context(tc.tile_pool(name="codep", bufs=6))
-        normp = ctx.enter_context(tc.tile_pool(name="normp", bufs=6))
-        gatep = ctx.enter_context(tc.tile_pool(name="gatep", bufs=2))
-        outp = ctx.enter_context(tc.tile_pool(name="outp", bufs=6))
-        psum = ctx.enter_context(tc.psum_pool(name="psum", bufs=8))
-        ctx.enter_context(tc.manual_schedule())
-
+        rawp = ctx.enter_context(tc.tile_pool(name="rawp", bufs=RAW_BUFS))
+        grpp = ctx.enter_context(tc.tile_pool(name="grpp", bufs=GROUPED_BUFS))
+        codep = ctx.enter_context(tc.tile_pool(name="codep", bufs=CODE_BUFS))
+        normp = ctx.enter_context(tc.tile_pool(name="normp", bufs=NORM_BUFS))
+        gatep = ctx.enter_context(tc.tile_pool(name="gatep", bufs=GATE_BUFS))
+        outp = ctx.enter_context(tc.tile_pool(name="outp", bufs=OUT_BUFS))
+        psum = ctx.enter_context(tc.psum_pool(name="psum", bufs=PSUM_BANKS))
 
         ident = const.tile([P, P], F32, name="ident")
         make_identity(nc, ident[:])
@@ -86,73 +65,77 @@ def tile_multiscaleretention_pb_kernel(tc, x, attn, Wg, bg, gn_w, gn_b, Wo, bo, 
         nc.vector.memset(vraw[:], 0.0)
         eps_t = const.tile([P, 1], F32, name="eps_t")
         nc.vector.memset(eps_t[:], EPS)
-        nc.scalar.dma_start(out=vraw[0:16, :], in_=bg.rearrange("(r c) -> r c", c=P))
-        nc.scalar.dma_start(out=vraw[16:32, :], in_=gn_w.rearrange("(r c) -> r c", c=P))
-        nc.scalar.dma_start(out=vraw[32:48, :], in_=gn_b.rearrange("(r c) -> r c", c=P))
+        nc.scalar.dma_start(out=vraw[0:GROUPS, :], in_=bg.rearrange("(r c) -> r c", c=P))
+        nc.scalar.dma_start(out=vraw[GROUPS:2 * GROUPS, :], in_=gn_w.rearrange("(r c) -> r c", c=P))
+        nc.scalar.dma_start(out=vraw[2 * GROUPS:3 * GROUPS, :], in_=gn_b.rearrange("(r c) -> r c", c=P))
         warm = const.tile([P, 1], F32, name="warm")
         nc.scalar.activation(out=warm[:], in_=eps_t[:], func=ACT.Sqrt, scale=1.0)
 
         bo_bc = const.tile([P, E], BF16, name="bo_bc")
         vf = const.tile([P, P], F32, name="vf")
-        vcol = const.tile([P, 48], F32, name="vcol")
-        st = const.tile([P, 64, 6], F32, name="st")
-        dif = const.tile([P, 64], F32, name="dif")
-        mu = const.tile([P, 64], F32, name="mu")
-        m2 = const.tile([P, 64], F32, name="m2")
-        std = const.tile([P, 64], F32, name="std")
-        rstd = const.tile([P, 64], F32, name="rstd")
-        xc = const.tile([P, NPASS, S], U32, name="xc", align_bytes=64)
-        xs = const.tile([P, NPASS, S], U8, name="xs", align_bytes=64)
-        hc = const.tile([P, NPASS, S], U32, name="hc", align_bytes=64)
-        hs = const.tile([P, NPASS, S], U8, name="hs", align_bytes=64)
-        T = {}
+        vcol = const.tile([P, 3 * GROUPS], F32, name="vcol")
+        st = const.tile([P, TILES * GROUPS, 6], F32, name="st")
+        dif = const.tile([P, TILES * GROUPS], F32, name="dif")
+        mu = const.tile([P, TILES * GROUPS], F32, name="mu")
+        m2 = const.tile([P, TILES * GROUPS], F32, name="m2")
+        std = const.tile([P, TILES * GROUPS], F32, name="std")
+        rstd = const.tile([P, TILES * GROUPS], F32, name="rstd")
+        xc = const.tile([P, PASSES, S], U32, name="xc", align_bytes=64)
+        xs = const.tile([P, PASSES, S], U8, name="xs", align_bytes=64)
+        hc = const.tile([P, PASSES, S], U32, name="hc", align_bytes=64)
+        hs = const.tile([P, PASSES, S], U8, name="hs", align_bytes=64)
+        tiles = {}
 
-        def ld_attn(s):
-            T[("a", s)] = const.tile([P, E], BF16, name="a_sb%d" % s)
+        def load_attn(s):
+            tiles[("a", s)] = const.tile([P, E], BF16, name="a_sb%d" % s)
             cuts = 2 if s == 0 else 1
-            w = E // cuts
+            width = E // cuts
             for i in range(cuts):
-                nc.sync.dma_start(out=T[("a", s)][:, w * i:w * i + w], in_=af[P * s:P * s + P, w * i:w * i + w])
+                cols = slice(width * i, width * i + width)
+                nc.sync.dma_start(out=tiles[("a", s)][:, cols], in_=af[P * s:P * s + P, cols])
 
-        def ld_raw(kind, a, c):
-            t = rawp.tile([P, 4096], BF16, name="raw_%s%d%d" % (kind, a, c), tag="raw")
-            T[("raw", kind, a, c)] = t
+        def load(kind, part, c):
+            raw = rawp.tile([P, PACK * LOAD_COLS], BF16, name="raw_%s%d%d" % (kind, part, c), tag="raw")
+            tiles[("raw", kind, part, c)] = raw
             if kind == "x":
                 nc.sync.dma_start(
-                    out=t[:].rearrange("p (s k) -> p s k", s=2),
-                    in_=xf[256 * a:256 * a + 256, :].rearrange("(s p) k -> p s k", p=P),
+                    out=raw[:].rearrange("p (s k) -> p s k", s=2),
+                    in_=xf[2 * P * part:2 * P * part + 2 * P, :].rearrange("(s p) k -> p s k", p=P),
                 )
             elif kind == "g":
-                tv = t[:].rearrange("p (t c) -> p t c", t=4)
-                cuts = 2 if (a == 0 and c == 0) else 1
-                w = 1024 // cuts
+                rows = raw[:].rearrange("p (t c) -> p t c", t=PACK)
+                cuts = 2 if (part == 0 and c == 0) else 1
+                width = LOAD_COLS // cuts
                 for i in range(cuts):
                     for u in range(2):
-                        r0 = 512 * c + 256 * u
-                        c0 = 1024 * a + w * i
+                        r0 = K_PASS * c + K_HALF * u
+                        c0 = LOAD_COLS * part + width * i
                         nc.sync.dma_start(
-                            out=tv[:, 2 * u:2 * u + 2, w * i:w * i + w],
-                            in_=Wg[r0:r0 + 256, c0:c0 + w].rearrange("(q e) c -> q e c", e=2),
+                            out=rows[:, 2 * u:2 * u + 2, width * i:width * i + width],
+                            in_=Wg[r0:r0 + K_HALF, c0:c0 + width].rearrange("(q e) c -> q e c", e=2),
                         )
             else:
+                r0 = K_PASS * c
+                c0 = LOAD_COLS * part
                 nc.sync.dma_start(
-                    out=t[:].rearrange("p (t c) -> p t c", t=4),
-                    in_=Wo[512 * c:512 * c + 512, 1024 * a:1024 * a + 1024].rearrange("(t p) c -> p t c", p=P),
+                    out=raw[:].rearrange("p (t c) -> p t c", t=PACK),
+                    in_=Wo[r0:r0 + K_PASS, c0:c0 + LOAD_COLS].rearrange("(t p) c -> p t c", p=P),
                 )
 
-        def vec_prep():
+        def load_bo():
+            nc.sync.dma_start(out=bo_bc[:], in_=bo.partition_broadcast(P))
+
+        def vectors():
             nc.vector.tensor_copy(out=vf[:], in_=vraw[:])
             vt = psum.tile([P, P], F32, name="vt", tag="ps")
             nc.tensor.transpose(vt[:], vf[:], ident[:])
-            nc.vector.tensor_copy(out=vcol[:], in_=vt[:, 0:48])
+            nc.vector.tensor_copy(out=vcol[:], in_=vt[:, 0:3 * GROUPS])
 
-        def bn(s):
-            for g in range(16):
-                nc.vector.bn_stats(out=st[:, 16 * s + g, :], in_=T[("a", s)][:, P * g:P * g + P])
-            if s == 0:
-                vec_prep()
+        def stats(s):
+            for g in range(GROUPS):
+                nc.vector.bn_stats(out=st[:, GROUPS * s + g, :], in_=tiles[("a", s)][:, P * g:P * g + P])
 
-        def small():
+        def moments():
             me, m2e, mo, m2o = st[:, :, 1], st[:, :, 2], st[:, :, 4], st[:, :, 5]
             nc.vector.tensor_tensor(out=dif[:], in0=me, in1=mo, op=ALU.subtract)
             nc.vector.tensor_tensor(out=mu[:], in0=me, in1=mo, op=ALU.add)
@@ -163,55 +146,65 @@ def tile_multiscaleretention_pb_kernel(tc, x, attn, Wg, bg, gn_w, gn_b, Wo, bo, 
                 out=m2[:], in0=dif[:], scalar=32.0, in1=m2[:], op0=ALU.mult, op1=ALU.add
             )
 
-        def x_transpose(g, sp):
-            xt = psum.tile([P, 2, 256], F32, name="xt%d%d" % (g, sp), tag="ps")
-            T[("xt", g, sp)] = xt
-            xw = T[("raw", "x", sp, 0)][:].bitcast(F32)
-            for u in range(2):
-                for sl in range(2):
-                    c0 = 1024 * sl + 256 * g + P * u
-                    nc.tensor.transpose(xt[:, u, P * sl:P * sl + P], xw[:, c0:c0 + P], ident[:])
+        def std_dev():
+            nc.scalar.activation(out=std[:], in_=m2[:], func=ACT.Sqrt, bias=eps_t[:, 0:1], scale=1.0 / P)
 
-        def x_evac(g, sp):
-            if ("xq", g) not in T:
-                T[("xq", g)] = grpp.tile([P, 2048], BF16, name="xq%d" % g, tag="grp", align_bytes=64)
-            xq32 = T[("xq", g)][:].bitcast(F32).rearrange("p (r u) -> p r u", u=2)
+        def inverse_std():
+            nc.vector.reciprocal(out=rstd[:], in_=std[:])
+
+        def x_transpose(c, part):
+            xt = psum.tile([P, 2, 2 * P], F32, name="xt%d%d" % (c, part), tag="ps")
+            tiles[("xt", c, part)] = xt
+            pairs = tiles[("raw", "x", part, 0)][:].bitcast(F32)
+            for u in range(2):
+                for j in range(2):
+                    w0 = (E // 2) * j + K_HALF * c + P * u
+                    nc.tensor.transpose(xt[:, u, P * j:P * j + P], pairs[:, w0:w0 + P], ident[:])
+
+        def x_regroup(c, part):
+            if ("xq", c) not in tiles:
+                tiles[("xq", c)] = grpp.tile([P, PACK * S], BF16, name="xq%d" % c, tag="grp", align_bytes=64)
+            xq32 = tiles[("xq", c)][:].bitcast(F32).rearrange("p (r u) -> p r u", u=2)
             nc.scalar.copy(
-                out=xq32[:, 256 * sp:256 * sp + 256, :], in_=T[("xt", g, sp)][:].rearrange("p u r -> p r u")
+                out=xq32[:, 2 * P * part:2 * P * part + 2 * P, :],
+                in_=tiles[("xt", c, part)][:].rearrange("p u r -> p r u"),
             )
 
-        def regroup(eng, kind, blk, c):
-            raw = T[("raw", kind, blk // 2, c)]
-            col0 = 512 * (blk % 2)
-            src = raw[:].rearrange("p (t c) -> p t c", t=4)[:, :, col0:col0 + 512]
-            g4 = grpp.tile([P, 2048], BF16, name="g4_%s%d%d" % (kind, blk, c), tag="grp", align_bytes=64)
-            T[("g4", kind, blk, c)] = g4
-            dst = g4[:].rearrange("p (c i t) -> p c t i", i=4, t=4)
-            srcv = src.rearrange("p t (c i) -> p c t i", i=4)
-            if eng == "V":
-                nc.vector.tensor_copy(out=dst, in_=srcv)
-            else:
-                nc.scalar.copy(out=dst, in_=srcv)
+        def x_quantise(c):
+            nc.vector.quantize_mx(out=xc[:, c, :].bitcast(FP8X4), scales=xs[:, c, :], in_=tiles[("xq", c)][:])
 
-        def quant(kind, blk, c):
-            if ("wc", kind, blk) not in T:
-                T[("wc", kind, blk)] = codep.tile(
-                    [P, NPASS, 512], U32, name="wc_%s%d" % (kind, blk), tag="wc", align_bytes=64
+        def regroup(engine, kind, panel, c):
+            raw = tiles[("raw", kind, panel // 2, c)]
+            c0 = PANEL * (panel % 2)
+            src = raw[:].rearrange("p (t c) -> p t c", t=PACK)[:, :, c0:c0 + PANEL]
+            g4 = grpp.tile([P, PACK * PANEL], BF16, name="g4_%s%d%d" % (kind, panel, c), tag="grp", align_bytes=64)
+            tiles[("g4", kind, panel, c)] = g4
+            dst = g4[:].rearrange("p (c i t) -> p c t i", i=RUN, t=PACK)
+            runs = src.rearrange("p t (c i) -> p c t i", i=RUN)
+            if engine == "V":
+                nc.vector.tensor_copy(out=dst, in_=runs)
+            else:
+                nc.scalar.copy(out=dst, in_=runs)
+
+        def quantise(kind, panel, c):
+            if ("wc", kind, panel) not in tiles:
+                tiles[("wc", kind, panel)] = codep.tile(
+                    [P, PASSES, PANEL], U32, name="wc_%s%d" % (kind, panel), tag="wc", align_bytes=64
                 )
-                T[("ws", kind, blk)] = codep.tile(
-                    [P, NPASS, 512], U8, name="ws_%s%d" % (kind, blk), tag="ws", align_bytes=64
+                tiles[("ws", kind, panel)] = codep.tile(
+                    [P, PASSES, PANEL], U8, name="ws_%s%d" % (kind, panel), tag="ws", align_bytes=64
                 )
             nc.vector.quantize_mx(
-                out=T[("wc", kind, blk)][:, c, :].bitcast(FP8X4),
-                scales=T[("ws", kind, blk)][:, c, :],
-                in_=T[("g4", kind, blk, c)][:],
+                out=tiles[("wc", kind, panel)][:, c, :].bitcast(FP8X4),
+                scales=tiles[("ws", kind, panel)][:, c, :],
+                in_=tiles[("g4", kind, panel, c)][:],
             )
 
-        def mx1(G, t):
-            z = psum.tile([P, S], F32, name="z%d%d" % (G, t), tag="ps")
-            T[("z", G, t)] = z
-            wc, ws = T[("wc", "g", G)], T[("ws", "g", G)]
-            for c in range(NPASS):
+        def stage1(panel, t):
+            z = psum.tile([P, S], F32, name="z%d%d" % (panel, t), tag="ps")
+            tiles[("z", panel, t)] = z
+            wc, ws = tiles[("wc", "g", panel)], tiles[("ws", "g", panel)]
+            for c in range(PASSES):
                 nc.tensor.matmul_mx(
                     out=z[:],
                     lhsT=wc[:, c, P * t:P * t + P].bitcast(FP8X4),
@@ -219,135 +212,193 @@ def tile_multiscaleretention_pb_kernel(tc, x, attn, Wg, bg, gn_w, gn_b, Wo, bo, 
                     rhs=xc[:, c, :].bitcast(FP8X4),
                     rhs_scale=xs[:, c, :],
                     start=(c == 0),
-                    stop=(c == NPASS - 1),
+                    stop=(c == PASSES - 1),
                 )
 
-        def normalise(G, s):
-            nrm = normp.tile([P, 512], F32, name="nrm%d%d" % (G, s), tag="nrm")
-            T[("nrm", G, s)] = nrm
-            for t in range(4):
-                gi = 4 * G + t
-                k = 16 * s + gi
+        def normalise(panel, s):
+            nrm = normp.tile([P, PANEL], F32, name="nrm%d%d" % (panel, s), tag="nrm")
+            tiles[("nrm", panel, s)] = nrm
+            for t in range(TILES):
+                g = TILES * panel + t
+                k = GROUPS * s + g
                 nc.vector.tensor_scalar(
                     out=nrm[:, P * t:P * t + P],
-                    in0=T[("a", s)][:, P * gi:P * gi + P],
+                    in0=tiles[("a", s)][:, P * g:P * g + P],
                     scalar1=mu[:, k:k + 1],
                     scalar2=rstd[:, k:k + 1],
                     op0=ALU.subtract,
                     op1=ALU.mult,
                 )
 
-        def n_transpose(G, t):
-            nT = psum.tile([P, S], F32, name="nT%d%d" % (G, t), tag="ps")
-            T[("nT", G, t)] = nT
-            for s in range(4):
-                nc.tensor.transpose(nT[:, P * s:P * s + P], T[("nrm", G, s)][:, P * t:P * t + P], ident[:])
+        def n_transpose(panel, t):
+            nT = psum.tile([P, S], F32, name="nT%d%d" % (panel, t), tag="ps")
+            tiles[("nT", panel, t)] = nT
+            for s in range(TILES):
+                nc.tensor.transpose(nT[:, P * s:P * s + P], tiles[("nrm", panel, s)][:, P * t:P * t + P], ident[:])
 
-        def silu(G, t):
-            if ("sil", G) not in T:
-                T[("sil", G)] = gatep.tile([P, 2048], F32, name="sil%d" % G, tag="sil")
-            gi = 4 * G + t
+        def silu(panel, t):
+            if ("sil", panel) not in tiles:
+                tiles[("sil", panel)] = gatep.tile([P, TILES * S], F32, name="sil%d" % panel, tag="sil")
+            g = TILES * panel + t
             nc.scalar.activation(
-                out=T[("sil", G)][:, S * t:S * t + S], in_=T[("z", G, t)][:], func=ACT.Silu,
-                bias=vcol[:, gi:gi + 1], scale=1.0,
+                out=tiles[("sil", panel)][:, S * t:S * t + S], in_=tiles[("z", panel, t)][:], func=ACT.Silu,
+                bias=vcol[:, g:g + 1], scale=1.0,
             )
 
-        def gain(G, t):
-            if ("gw", G) not in T:
-                T[("gw", G)] = gatep.tile([P, 2048], F32, name="gw%d" % G, tag="gw")
-            gi = 4 * G + t
+        def gain(panel, t):
+            if ("gw", panel) not in tiles:
+                tiles[("gw", panel)] = gatep.tile([P, TILES * S], F32, name="gw%d" % panel, tag="gw")
+            g = TILES * panel + t
             nc.scalar.activation(
-                out=T[("gw", G)][:, S * t:S * t + S], in_=T[("nT", G, t)][:], func=ACT.Identity,
-                bias=vcol[:, 32 + gi:33 + gi], scale=vcol[:, 16 + gi:17 + gi],
+                out=tiles[("gw", panel)][:, S * t:S * t + S], in_=tiles[("nT", panel, t)][:], func=ACT.Identity,
+                bias=vcol[:, 2 * GROUPS + g:2 * GROUPS + g + 1], scale=vcol[:, GROUPS + g:GROUPS + g + 1],
             )
 
-        def gate_mul(G):
-            hq = grpp.tile([P, 2048], BF16, name="hq%d" % G, tag="grp", align_bytes=64)
-            T[("hq", G)] = hq
+        def gate(panel):
+            hq = grpp.tile([P, PACK * S], BF16, name="hq%d" % panel, tag="grp", align_bytes=64)
+            tiles[("hq", panel)] = hq
             nc.vector.tensor_tensor(
-                out=hq[:].rearrange("p (c i t) -> p c t i", i=4, t=4),
-                in0=T[("sil", G)][:].rearrange("p (t c i) -> p c t i", t=4, i=4),
-                in1=T[("gw", G)][:].rearrange("p (t c i) -> p c t i", t=4, i=4),
+                out=hq[:].rearrange("p (c i t) -> p c t i", i=RUN, t=PACK),
+                in0=tiles[("sil", panel)][:].rearrange("p (t c i) -> p c t i", t=PACK, i=RUN),
+                in1=tiles[("gw", panel)][:].rearrange("p (t c i) -> p c t i", t=PACK, i=RUN),
                 op=ALU.mult,
             )
 
-        def mx2(NB, G):
-            if G == 0:
-                for s in range(4):
-                    T[("acc", NB, s)] = psum.tile(
-                        [P, 512], F32, name="acc%d%d" % (NB, s), tag="ps"
-                    )
-            wc, ws = T[("wc", "o", NB)], T[("ws", "o", NB)]
-            for s in range(4):
+        def h_quantise(c):
+            nc.vector.quantize_mx(out=hc[:, c, :].bitcast(FP8X4), scales=hs[:, c, :], in_=tiles[("hq", c)][:])
+
+        def stage2(panel, c):
+            if c == 0:
+                for s in range(TILES):
+                    tiles[("acc", panel, s)] = psum.tile([P, PANEL], F32, name="acc%d%d" % (panel, s), tag="ps")
+            wc, ws = tiles[("wc", "o", panel)], tiles[("ws", "o", panel)]
+            for s in range(TILES):
                 nc.tensor.matmul_mx(
-                    out=T[("acc", NB, s)][:],
-                    lhsT=hc[:, G, P * s:P * s + P].bitcast(FP8X4),
-                    lhsT_scale=hs[:, G, P * s:P * s + P],
-                    rhs=wc[:, G, :].bitcast(FP8X4),
-                    rhs_scale=ws[:, G, :],
-                    start=(G == 0),
-                    stop=(G == NPASS - 1),
+                    out=tiles[("acc", panel, s)][:],
+                    lhsT=hc[:, c, P * s:P * s + P].bitcast(FP8X4),
+                    lhsT_scale=hs[:, c, P * s:P * s + P],
+                    rhs=wc[:, c, :].bitcast(FP8X4),
+                    rhs_scale=ws[:, c, :],
+                    start=(c == 0),
+                    stop=(c == PASSES - 1),
                 )
 
-        def bias_out(NB, s):
-            o_sb = outp.tile([P, 512], F32, name="o%d%d" % (NB, s), tag="o")
-            T[("o", NB, s)] = o_sb
-            nc.vector.tensor_tensor(
-                out=o_sb[:], in0=T[("acc", NB, s)][:], in1=bo_bc[:, 512 * NB:512 * NB + 512], op=ALU.add
-            )
+        def bias(panel, s):
+            o_sb = outp.tile([P, PANEL], F32, name="o%d%d" % (panel, s), tag="o")
+            tiles[("o", panel, s)] = o_sb
+            cols = slice(PANEL * panel, PANEL * panel + PANEL)
+            nc.vector.tensor_tensor(out=o_sb[:], in0=tiles[("acc", panel, s)][:], in1=bo_bc[:, cols], op=ALU.add)
 
-        for tok in ORDER:
-            k = tok[0]
-            if k == "ldA":
-                ld_attn(tok[1])
-            elif k == "ld":
-                ld_raw(tok[1], tok[2], tok[3])
-            elif k == "ldbo":
-                nc.sync.dma_start(out=bo_bc[:], in_=bo.partition_broadcast(P))
-            elif k == "bn":
-                bn(tok[1])
-            elif k == "sm":
-                small()
-            elif k == "sqrt":
-                nc.scalar.activation(out=std[:], in_=m2[:], func=ACT.Sqrt, bias=eps_t[:, 0:1], scale=1.0 / P)
-            elif k == "recip":
-                nc.vector.reciprocal(out=rstd[:], in_=std[:])
-            elif k == "xT":
-                x_transpose(tok[1], tok[2])
-            elif k == "XE":
-                x_evac(tok[1], tok[2])
-            elif k == "Qx":
-                nc.vector.quantize_mx(
-                    out=xc[:, tok[1], :].bitcast(FP8X4), scales=xs[:, tok[1], :], in_=T[("xq", tok[1])][:]
-                )
-            elif k == "RGV":
-                regroup("V", tok[1], tok[2], tok[3])
-            elif k == "RGS":
-                regroup("S", tok[1], tok[2], tok[3])
-            elif k == "Q":
-                quant(tok[1], tok[2], tok[3])
-            elif k == "MX1":
-                mx1(tok[1], tok[2])
-            elif k == "J4":
-                normalise(tok[1], tok[2])
-            elif k == "T":
-                n_transpose(tok[1], tok[2])
-            elif k == "SIL":
-                silu(tok[1], tok[2])
-            elif k == "GW":
-                gain(tok[1], tok[2])
-            elif k == "MUL":
-                gate_mul(tok[1])
-            elif k == "QH":
-                nc.vector.quantize_mx(
-                    out=hc[:, tok[1], :].bitcast(FP8X4), scales=hs[:, tok[1], :], in_=T[("hq", tok[1])][:]
-                )
-            elif k == "MX2":
-                mx2(tok[1], tok[2])
-            elif k == "J5":
-                bias_out(tok[1], tok[2])
-            elif k == "st":
-                NB, s = tok[1], tok[2]
-                nc.sync.dma_start(out=of[P * s:P * s + P, 512 * NB:512 * NB + 512], in_=T[("o", NB, s)][:])
-            else:
-                assert False, k
+        def store(panel, s):
+            cols = slice(PANEL * panel, PANEL * panel + PANEL)
+            nc.sync.dma_start(out=of[P * s:P * s + P, cols], in_=tiles[("o", panel, s)][:])
+
+        def load_next():
+            kind, part, c = loads[cursor["load"]]
+            cursor["load"] = cursor["load"] + 1
+            load(kind, part, c)
+
+        def regroup_and_refill(kind, panel, c):
+            regroup("V" if on_vector(kind, panel, c) else "S", kind, panel, c)
+            if panel % 2 == 1 and cursor["load"] < len(loads):
+                load_next()
+
+        def bias_and_store(panel):
+            for s in range(TILES):
+                bias(panel, s)
+                store(panel, s)
+
+        loads = [("g", 0, c) for c in range(PASSES)] + [("x", 0, 0), ("x", 1, 0)]
+        loads += [("g", 1, c) for c in range(PASSES)]
+        loads += [("o", part, c) for part in range(2) for c in range(PASSES)]
+        cursor = {"load": 0}
+
+        for s in range(TILES):
+            load_attn(s)
+            load_next()
+        load_next()
+        load_next()
+        for c in range(PASSES):
+            stats(c)
+            if c == 0:
+                vectors()
+            for panel in range(2):
+                regroup_and_refill("g", panel, c)
+            if c > 0:
+                for panel in range(2):
+                    quantise("g", panel, c - 1)
+        moments()
+        std_dev()
+        for panel in range(2):
+            quantise("g", panel, PASSES - 1)
+        inverse_std()
+        for part in range(2):
+            for c in range(PASSES):
+                x_transpose(c, part)
+        for s in range(TILES):
+            normalise(0, s)
+        for part in range(2):
+            for c in range(PASSES):
+                x_regroup(c, part)
+        load_bo()
+        load_next()
+        load_next()
+        for t in range(TILES):
+            n_transpose(0, t)
+        for s in range(TILES):
+            normalise(1, s)
+        for c in range(PASSES):
+            x_quantise(c)
+
+        ahead = [("g", 2), ("g", 3), ("o", 0), ("o", 1)]
+        for r in range(PASSES):
+            kind, panel = ahead[r]
+            vector_units = [c for c in range(PASSES) if on_vector(kind, panel, c)]
+            scalar_units = [c for c in range(PASSES) if not on_vector(kind, panel, c)]
+            for t in range(TILES):
+                gain(r, t)
+            for t in range(TILES):
+                stage1(r, t)
+            if r + 1 < PASSES:
+                for t in range(TILES):
+                    n_transpose(r + 1, t)
+            if r > 0:
+                gate(r - 1)
+                h_quantise(r - 1)
+            if r == PASSES - 1:
+                for c in range(r):
+                    stage2(0, c)
+            regroup_and_refill(kind, panel, scalar_units[0])
+            for t in range(TILES):
+                silu(r, t)
+            for c in scalar_units[1:]:
+                regroup_and_refill(kind, panel, c)
+            for i, c in enumerate(vector_units):
+                regroup_and_refill(kind, panel, c)
+                if i > 0:
+                    quantise(kind, panel, vector_units[i - 1])
+            if r + 2 < PASSES:
+                for s in range(TILES):
+                    normalise(r + 2, s)
+            quantise(kind, panel, vector_units[-1])
+            for c in scalar_units:
+                quantise(kind, panel, c)
+
+        for c in range(PASSES - 1):
+            stage2(1, c)
+        gate(PASSES - 1)
+        h_quantise(PASSES - 1)
+        for panel in range(2):
+            stage2(panel, PASSES - 1)
+        for panel in range(2, 4):
+            vector_units = [c for c in range(PASSES) if on_vector("o", panel, c)]
+            scalar_units = [c for c in range(PASSES) if not on_vector("o", panel, c)]
+            for c in scalar_units + vector_units:
+                regroup_and_refill("o", panel, c)
+            bias_and_store(panel - 2)
+            for c in vector_units + scalar_units:
+                quantise("o", panel, c)
+            for c in range(PASSES):
+                stage2(panel, c)
+        for panel in range(2, 4):
+            bias_and_store(panel)

from contextlib import ExitStack

import concourse.mybir as mybir
from concourse.masks import make_identity

F32 = mybir.dt.float32
BF16 = mybir.dt.bfloat16
U32 = mybir.dt.uint32
U8 = mybir.dt.uint8
FP8X4 = mybir.dt.float8_e4m3fn_x4
ALU = mybir.AluOpType
ACT = mybir.ActivationFunctionType

P = 128
S = 512
E = 2048
EPS = 1e-5
PACK = 4
K_PASS = P * PACK
K_HALF = K_PASS // 2
PASSES = E // K_PASS
PANEL = 512
TILES = 4
GROUPS = E // P
LOAD_COLS = 2 * PANEL
RUN = 4
FLOPS = 2 * 2 * S * E * E

RAW_BUFS = 6
GROUPED_BUFS = 5
CODE_BUFS = 6
NORM_BUFS = 8
GATE_BUFS = 2
OUT_BUFS = 6
PSUM_BANKS = 8


def on_vector(kind, panel, c):
    if kind == "g" and panel < 2:
        return c == PASSES - 1
    if kind == "g" or panel < 2:
        return c < PASSES - 1
    return panel == 2 and c < 2


def tile_multiscaleretention_pb_kernel(tc, x, attn, Wg, bg, gn_w, gn_b, Wo, bo, out):
    nc = tc.nc
    xf = x.flatten_outer_dims()
    af = attn.flatten_outer_dims()
    of = out.flatten_outer_dims()

    with ExitStack() as ctx:
        const = ctx.enter_context(tc.tile_pool(name="const", bufs=1))
        rawp = ctx.enter_context(tc.tile_pool(name="rawp", bufs=RAW_BUFS))
        grpp = ctx.enter_context(tc.tile_pool(name="grpp", bufs=GROUPED_BUFS))
        codep = ctx.enter_context(tc.tile_pool(name="codep", bufs=CODE_BUFS))
        normp = ctx.enter_context(tc.tile_pool(name="normp", bufs=NORM_BUFS))
        gatep = ctx.enter_context(tc.tile_pool(name="gatep", bufs=GATE_BUFS))
        outp = ctx.enter_context(tc.tile_pool(name="outp", bufs=OUT_BUFS))
        psum = ctx.enter_context(tc.psum_pool(name="psum", bufs=PSUM_BANKS))

        ident = const.tile([P, P], F32, name="ident")
        make_identity(nc, ident[:])
        vraw = const.tile([P, P], BF16, name="vraw")
        nc.vector.memset(vraw[:], 0.0)
        eps_t = const.tile([P, 1], F32, name="eps_t")
        nc.vector.memset(eps_t[:], EPS)
        nc.scalar.dma_start(out=vraw[0:GROUPS, :], in_=bg.rearrange("(r c) -> r c", c=P))
        nc.scalar.dma_start(out=vraw[GROUPS:2 * GROUPS, :], in_=gn_w.rearrange("(r c) -> r c", c=P))
        nc.scalar.dma_start(out=vraw[2 * GROUPS:3 * GROUPS, :], in_=gn_b.rearrange("(r c) -> r c", c=P))
        warm = const.tile([P, 1], F32, name="warm")
        nc.scalar.activation(out=warm[:], in_=eps_t[:], func=ACT.Sqrt, scale=1.0)

        bo_bc = const.tile([P, E], BF16, name="bo_bc")
        vf = const.tile([P, P], F32, name="vf")
        vcol = const.tile([P, 3 * GROUPS], F32, name="vcol")
        st = const.tile([P, TILES * GROUPS, 6], F32, name="st")
        dif = const.tile([P, TILES * GROUPS], F32, name="dif")
        mu = const.tile([P, TILES * GROUPS], F32, name="mu")
        m2 = const.tile([P, TILES * GROUPS], F32, name="m2")
        std = const.tile([P, TILES * GROUPS], F32, name="std")
        rstd = const.tile([P, TILES * GROUPS], F32, name="rstd")
        xc = const.tile([P, PASSES, S], U32, name="xc", align_bytes=64)
        xs = const.tile([P, PASSES, S], U8, name="xs", align_bytes=64)
        hc = const.tile([P, PASSES, S], U32, name="hc", align_bytes=64)
        hs = const.tile([P, PASSES, S], U8, name="hs", align_bytes=64)
        tiles = {}

        def load_attn(s):
            tiles[("a", s)] = const.tile([P, E], BF16, name="a_sb%d" % s)
            cuts = 2 if s == 0 else 1
            width = E // cuts
            for i in range(cuts):
                cols = slice(width * i, width * i + width)
                nc.sync.dma_start(out=tiles[("a", s)][:, cols], in_=af[P * s:P * s + P, cols])

        def load(kind, part, c):
            raw = rawp.tile([P, PACK * LOAD_COLS], BF16, name="raw_%s%d%d" % (kind, part, c), tag="raw")
            tiles[("raw", kind, part, c)] = raw
            if kind == "x":
                nc.sync.dma_start(
                    out=raw[:].rearrange("p (s k) -> p s k", s=2),
                    in_=xf[2 * P * part:2 * P * part + 2 * P, :].rearrange("(s p) k -> p s k", p=P),
                )
            elif kind == "g":
                rows = raw[:].rearrange("p (t c) -> p t c", t=PACK)
                cuts = 2 if (part == 0 and c == 0) else 1
                width = LOAD_COLS // cuts
                for i in range(cuts):
                    for u in range(2):
                        r0 = K_PASS * c + K_HALF * u
                        c0 = LOAD_COLS * part + width * i
                        nc.sync.dma_start(
                            out=rows[:, 2 * u:2 * u + 2, width * i:width * i + width],
                            in_=Wg[r0:r0 + K_HALF, c0:c0 + width].rearrange("(q e) c -> q e c", e=2),
                        )
            else:
                r0 = K_PASS * c
                c0 = LOAD_COLS * part
                nc.sync.dma_start(
                    out=raw[:].rearrange("p (t c) -> p t c", t=PACK),
                    in_=Wo[r0:r0 + K_PASS, c0:c0 + LOAD_COLS].rearrange("(t p) c -> p t c", p=P),
                )

        def load_bo():
            nc.sync.dma_start(out=bo_bc[:], in_=bo.partition_broadcast(P))

        def vectors():
            nc.vector.tensor_copy(out=vf[:], in_=vraw[:])
            vt = psum.tile([P, P], F32, name="vt", tag="ps")
            nc.tensor.transpose(vt[:], vf[:], ident[:])
            nc.vector.tensor_copy(out=vcol[:], in_=vt[:, 0:3 * GROUPS])

        def stats(s):
            for g in range(GROUPS):
                nc.vector.bn_stats(out=st[:, GROUPS * s + g, :], in_=tiles[("a", s)][:, P * g:P * g + P])

        def moments():
            me, m2e, mo, m2o = st[:, :, 1], st[:, :, 2], st[:, :, 4], st[:, :, 5]
            nc.vector.tensor_tensor(out=dif[:], in0=me, in1=mo, op=ALU.subtract)
            nc.vector.tensor_tensor(out=mu[:], in0=me, in1=mo, op=ALU.add)
            nc.vector.tensor_tensor(out=m2[:], in0=m2e, in1=m2o, op=ALU.add)
            nc.vector.tensor_tensor(out=dif[:], in0=dif[:], in1=dif[:], op=ALU.mult)
            nc.vector.tensor_scalar(out=mu[:], in0=mu[:], scalar1=0.5, scalar2=None, op0=ALU.mult)
            nc.vector.scalar_tensor_tensor(
                out=m2[:], in0=dif[:], scalar=32.0, in1=m2[:], op0=ALU.mult, op1=ALU.add
            )

        def std_dev():
            nc.scalar.activation(out=std[:], in_=m2[:], func=ACT.Sqrt, bias=eps_t[:, 0:1], scale=1.0 / P)

        def inverse_std():
            nc.vector.reciprocal(out=rstd[:], in_=std[:])

        def x_transpose(c, part):
            xt = psum.tile([P, 2, 2 * P], F32, name="xt%d%d" % (c, part), tag="ps")
            tiles[("xt", c, part)] = xt
            pairs = tiles[("raw", "x", part, 0)][:].bitcast(F32)
            for u in range(2):
                for j in range(2):
                    w0 = (E // 2) * j + K_HALF * c + P * u
                    nc.tensor.transpose(xt[:, u, P * j:P * j + P], pairs[:, w0:w0 + P], ident[:])

        def x_regroup(c, part):
            if ("xq", c) not in tiles:
                tiles[("xq", c)] = grpp.tile([P, PACK * S], BF16, name="xq%d" % c, tag="grp", align_bytes=64)
            xq32 = tiles[("xq", c)][:].bitcast(F32).rearrange("p (r u) -> p r u", u=2)
            nc.scalar.copy(
                out=xq32[:, 2 * P * part:2 * P * part + 2 * P, :],
                in_=tiles[("xt", c, part)][:].rearrange("p u r -> p r u"),
            )

        def x_quantise(c):
            nc.vector.quantize_mx(out=xc[:, c, :].bitcast(FP8X4), scales=xs[:, c, :], in_=tiles[("xq", c)][:])

        def regroup(engine, kind, panel, c):
            raw = tiles[("raw", kind, panel // 2, c)]
            c0 = PANEL * (panel % 2)
            src = raw[:].rearrange("p (t c) -> p t c", t=PACK)[:, :, c0:c0 + PANEL]
            g4 = grpp.tile([P, PACK * PANEL], BF16, name="g4_%s%d%d" % (kind, panel, c), tag="grp", align_bytes=64)
            tiles[("g4", kind, panel, c)] = g4
            dst = g4[:].rearrange("p (c i t) -> p c t i", i=RUN, t=PACK)
            runs = src.rearrange("p t (c i) -> p c t i", i=RUN)
            if engine == "V":
                nc.vector.tensor_copy(out=dst, in_=runs)
            else:
                nc.scalar.copy(out=dst, in_=runs)

        def quantise(kind, panel, c):
            if ("wc", kind, panel) not in tiles:
                tiles[("wc", kind, panel)] = codep.tile(
                    [P, PASSES, PANEL], U32, name="wc_%s%d" % (kind, panel), tag="wc", align_bytes=64
                )
                tiles[("ws", kind, panel)] = codep.tile(
                    [P, PASSES, PANEL], U8, name="ws_%s%d" % (kind, panel), tag="ws", align_bytes=64
                )
            nc.vector.quantize_mx(
                out=tiles[("wc", kind, panel)][:, c, :].bitcast(FP8X4),
                scales=tiles[("ws", kind, panel)][:, c, :],
                in_=tiles[("g4", kind, panel, c)][:],
            )

        def stage1(panel, t):
            z = psum.tile([P, S], F32, name="z%d%d" % (panel, t), tag="ps")
            tiles[("z", panel, t)] = z
            wc, ws = tiles[("wc", "g", panel)], tiles[("ws", "g", panel)]
            for c in range(PASSES):
                nc.tensor.matmul_mx(
                    out=z[:],
                    lhsT=wc[:, c, P * t:P * t + P].bitcast(FP8X4),
                    lhsT_scale=ws[:, c, P * t:P * t + P],
                    rhs=xc[:, c, :].bitcast(FP8X4),
                    rhs_scale=xs[:, c, :],
                    start=(c == 0),
                    stop=(c == PASSES - 1),
                )

        def normalise(panel, s):
            nrm = normp.tile([P, PANEL], F32, name="nrm%d%d" % (panel, s), tag="nrm")
            tiles[("nrm", panel, s)] = nrm
            for t in range(TILES):
                g = TILES * panel + t
                k = GROUPS * s + g
                nc.vector.tensor_scalar(
                    out=nrm[:, P * t:P * t + P],
                    in0=tiles[("a", s)][:, P * g:P * g + P],
                    scalar1=mu[:, k:k + 1],
                    scalar2=rstd[:, k:k + 1],
                    op0=ALU.subtract,
                    op1=ALU.mult,
                )

        def n_transpose(panel, t):
            nT = psum.tile([P, S], F32, name="nT%d%d" % (panel, t), tag="ps")
            tiles[("nT", panel, t)] = nT
            for s in range(TILES):
                nc.tensor.transpose(nT[:, P * s:P * s + P], tiles[("nrm", panel, s)][:, P * t:P * t + P], ident[:])

        def silu(panel, t):
            if ("sil", panel) not in tiles:
                tiles[("sil", panel)] = gatep.tile([P, TILES * S], F32, name="sil%d" % panel, tag="sil")
            g = TILES * panel + t
            nc.scalar.activation(
                out=tiles[("sil", panel)][:, S * t:S * t + S], in_=tiles[("z", panel, t)][:], func=ACT.Silu,
                bias=vcol[:, g:g + 1], scale=1.0,
            )

        def gain(panel, t):
            if ("gw", panel) not in tiles:
                tiles[("gw", panel)] = gatep.tile([P, TILES * S], F32, name="gw%d" % panel, tag="gw")
            g = TILES * panel + t
            nc.scalar.activation(
                out=tiles[("gw", panel)][:, S * t:S * t + S], in_=tiles[("nT", panel, t)][:], func=ACT.Identity,
                bias=vcol[:, 2 * GROUPS + g:2 * GROUPS + g + 1], scale=vcol[:, GROUPS + g:GROUPS + g + 1],
            )

        def gate(panel):
            hq = grpp.tile([P, PACK * S], BF16, name="hq%d" % panel, tag="grp", align_bytes=64)
            tiles[("hq", panel)] = hq
            nc.vector.tensor_tensor(
                out=hq[:].rearrange("p (c i t) -> p c t i", i=RUN, t=PACK),
                in0=tiles[("sil", panel)][:].rearrange("p (t c i) -> p c t i", t=PACK, i=RUN),
                in1=tiles[("gw", panel)][:].rearrange("p (t c i) -> p c t i", t=PACK, i=RUN),
                op=ALU.mult,
            )

        def h_quantise(c):
            nc.vector.quantize_mx(out=hc[:, c, :].bitcast(FP8X4), scales=hs[:, c, :], in_=tiles[("hq", c)][:])

        def stage2(panel, c):
            if c == 0:
                for s in range(TILES):
                    tiles[("acc", panel, s)] = psum.tile([P, PANEL], F32, name="acc%d%d" % (panel, s), tag="ps")
            wc, ws = tiles[("wc", "o", panel)], tiles[("ws", "o", panel)]
            for s in range(TILES):
                nc.tensor.matmul_mx(
                    out=tiles[("acc", panel, s)][:],
                    lhsT=hc[:, c, P * s:P * s + P].bitcast(FP8X4),
                    lhsT_scale=hs[:, c, P * s:P * s + P],
                    rhs=wc[:, c, :].bitcast(FP8X4),
                    rhs_scale=ws[:, c, :],
                    start=(c == 0),
                    stop=(c == PASSES - 1),
                )

        def bias(panel, s):
            o_sb = outp.tile([P, PANEL], F32, name="o%d%d" % (panel, s), tag="o")
            tiles[("o", panel, s)] = o_sb
            cols = slice(PANEL * panel, PANEL * panel + PANEL)
            nc.vector.tensor_tensor(out=o_sb[:], in0=tiles[("acc", panel, s)][:], in1=bo_bc[:, cols], op=ALU.add)

        def store(panel, s):
            cols = slice(PANEL * panel, PANEL * panel + PANEL)
            nc.sync.dma_start(out=of[P * s:P * s + P, cols], in_=tiles[("o", panel, s)][:])

        def load_next():
            kind, part, c = loads[cursor["load"]]
            cursor["load"] = cursor["load"] + 1
            load(kind, part, c)

        def regroup_and_refill(kind, panel, c):
            regroup("V" if on_vector(kind, panel, c) else "S", kind, panel, c)
            if panel % 2 == 1 and cursor["load"] < len(loads):
                load_next()

        def bias_and_store(panel):
            for s in range(TILES):
                bias(panel, s)
                store(panel, s)

        loads = [("g", 0, c) for c in range(PASSES)] + [("x", 0, 0), ("x", 1, 0)]
        loads += [("g", 1, c) for c in range(PASSES)]
        loads += [("o", part, c) for part in range(2) for c in range(PASSES)]
        cursor = {"load": 0}

        for s in range(TILES):
            load_attn(s)
            load_next()
        load_next()
        load_next()
        for c in range(PASSES):
            stats(c)
            if c == 0:
                vectors()
            for panel in range(2):
                regroup_and_refill("g", panel, c)
            if c > 0:
                for panel in range(2):
                    quantise("g", panel, c - 1)
        moments()
        std_dev()
        for panel in range(2):
            quantise("g", panel, PASSES - 1)
        inverse_std()
        for part in range(2):
            for c in range(PASSES):
                x_transpose(c, part)
        for s in range(TILES):
            normalise(0, s)
        for part in range(2):
            for c in range(PASSES):
                x_regroup(c, part)
        load_bo()
        load_next()
        load_next()
        for t in range(TILES):
            n_transpose(0, t)
        for s in range(TILES):
            normalise(1, s)
        for c in range(PASSES):
            x_quantise(c)

        ahead = [("g", 2), ("g", 3), ("o", 0), ("o", 1)]
        for r in range(PASSES):
            kind, panel = ahead[r]
            vector_units = [c for c in range(PASSES) if on_vector(kind, panel, c)]
            scalar_units = [c for c in range(PASSES) if not on_vector(kind, panel, c)]
            for t in range(TILES):
                gain(r, t)
            for t in range(TILES):
                stage1(r, t)
            if r + 1 < PASSES:
                for t in range(TILES):
                    n_transpose(r + 1, t)
            if r > 0:
                gate(r - 1)
                h_quantise(r - 1)
            if r == PASSES - 1:
                for c in range(r):
                    stage2(0, c)
            regroup_and_refill(kind, panel, scalar_units[0])
            for t in range(TILES):
                silu(r, t)
            for c in scalar_units[1:]:
                regroup_and_refill(kind, panel, c)
            for i, c in enumerate(vector_units):
                regroup_and_refill(kind, panel, c)
                if i > 0:
                    quantise(kind, panel, vector_units[i - 1])
            if r + 2 < PASSES:
                for s in range(TILES):
                    normalise(r + 2, s)
            quantise(kind, panel, vector_units[-1])
            for c in scalar_units:
                quantise(kind, panel, c)

        for c in range(PASSES - 1):
            stage2(1, c)
        gate(PASSES - 1)
        h_quantise(PASSES - 1)
        for panel in range(2):
            stage2(panel, PASSES - 1)
        for panel in range(2, 4):
            vector_units = [c for c in range(PASSES) if on_vector("o", panel, c)]
            scalar_units = [c for c in range(PASSES) if not on_vector("o", panel, c)]
            for c in scalar_units + vector_units:
                regroup_and_refill("o", panel, c)
            bias_and_store(panel - 2)
            for c in vector_units + scalar_units:
                quantise("o", panel, c)
            for c in range(PASSES):
                stage2(panel, c)
        for panel in range(2, 4):
            bias_and_store(panel)
